import numpy as np
import ml_dtypes


def mxq(x, axis, fmt="e4m3"):
    dtype, down = {"e4m3": (ml_dtypes.float8_e4m3fn, 7), "e5m2": (ml_dtypes.float8_e5m2, 14)}[fmt]
    v = np.moveaxis(np.asarray(x, np.float32).astype(ml_dtypes.bfloat16).astype(np.float64), axis, -1)
    blocks = v.reshape(v.shape[:-1] + (-1, 32))
    amax = np.abs(blocks).max(-1, keepdims=True)
    byte = np.maximum(np.where(amax > 0, np.frexp(amax)[1] - 1 + 127, 0) - down, 1)
    scale = np.exp2(byte - 127.0)
    codes = (blocks / scale).astype(np.float32).astype(dtype).astype(np.float64)
    return np.moveaxis((codes * scale).reshape(v.shape), -1, axis)


WIDE = False


def mx_kscale(k):
    if not WIDE:
        return np.ones(k)
    levels = np.array([10, -10, 5, -5, 0])
    a = np.random.permutation(np.resize(levels, k // 512 * 4)).reshape(k // 512, 4)
    idx = np.arange(k)
    return np.exp2(a[idx // 512, idx % 128 // 32])


BF16 = ml_dtypes.bfloat16


def bf(x):
    return np.asarray(x, np.float32).astype(BF16)


def f64(x):
    return np.asarray(x).astype(np.float64)


B, I, H = 128, 512, 512
QH = H % 512 == 0


def sigmoid(v):
    return 1.0 / (1.0 + np.exp(-v))


def setup_inputs():
    s = mx_kscale(I)
    t = mx_kscale(H) if QH else np.ones(H)
    n = np.random.standard_normal
    aw, ar = 0.6 / np.sqrt(I), 0.6 / np.sqrt(H)
    return {"xt": bf(n((B, I)) * s), "cx": bf(n((B, H))), "hx": bf(n((B, H)) * t),
            "w_fg": bf(n((H, I)) * aw / s), "w_ig": bf(n((H, I)) * aw / s), "w_og": bf(n((H, I)) * aw / s), "w_ci": bf(n((H, I)) * aw / s),
            "r_fg": bf(n((H, H)) * ar / t), "r_ig": bf(n((H, H)) * ar / t), "r_og": bf(n((H, H)) * ar / t), "r_ci": bf(n((H, H)) * ar / t),
            "b_fg": bf(n(H) * 0.3), "b_ig": bf(n(H) * 0.3), "b_og": bf(n(H) * 0.3), "b_ci": bf(n(H) * 0.3)}


def reference(xt, cx, hx, w_fg, w_ig, w_og, w_ci, r_fg, r_ig, r_og, r_ci, b_fg, b_ig, b_og, b_ci):
    W = np.concatenate([f64(w_fg), f64(w_ig), f64(w_og), f64(w_ci)], axis=0)
    R = np.concatenate([f64(r_fg), f64(r_ig), f64(r_og), f64(r_ci)], axis=0)
    b = np.concatenate([f64(b_fg), f64(b_ig), f64(b_og), f64(b_ci)], axis=0)
    gx = mxq(f64(xt), 1, "e4m3") @ mxq(W, 1, "e4m3").T
    if QH:
        gh = mxq(f64(hx), 1, "e4m3") @ mxq(R, 1, "e4m3").T
    else:
        gh = f64(hx) @ R.T
    gates = gx + gh + b
    f, i, o, g = np.split(gates, 4, axis=-1)
    ft = sigmoid(f)
    it = sigmoid(i)
    ot = sigmoid(o)
    ct = ft * f64(cx) + it * np.tanh(g)
    ht = ot * np.tanh(ct)
    return (ht, ct)

@@ -1,0 +1,167 @@
+from contextlib import ExitStack
+
+import concourse.mybir as mybir
+from concourse.masks import make_identity
+
+F32 = mybir.dt.float32
+BF16 = mybir.dt.bfloat16
+U32 = mybir.dt.uint32
+U8 = mybir.dt.uint8
+FP8X4 = mybir.dt.float8_e4m3fn_x4
+ACT = mybir.ActivationFunctionType
+ALU = mybir.AluOpType
+
+P = 128
+K = 512
+H = 512
+ROWS = 4
+HALVES = 2
+GATES = 4
+
+FLOPS = 2 * P * (K + K) * GATES * H
+
+
+def tile_lstmcell_s_kernel(
+    tc, xt, cx, hx, w_fg, w_ig, w_og, w_ci, r_fg, r_ig, r_og, r_ci, b_fg, b_ig, b_og, b_ci, out_0, out_1
+):
+    nc = tc.nc
+    gate_names = ["f", "i", "g", "o"]
+    gate_w = {"f": w_fg, "i": w_ig, "g": w_ci, "o": w_og}
+    gate_r = {"f": r_fg, "i": r_ig, "g": r_ci, "o": r_og}
+    gate_b = {"f": b_fg, "i": b_ig, "g": b_ci, "o": b_og}
+    gate_func = {"f": ACT.Sigmoid, "i": ACT.Sigmoid, "g": ACT.Tanh, "o": ACT.Sigmoid}
+
+    with ExitStack() as ctx:
+        keep = ctx.enter_context(tc.tile_pool(name="keep", bufs=1))
+        stage = ctx.enter_context(tc.tile_pool(name="stage", bufs=3))
+        work = ctx.enter_context(tc.tile_pool(name="work", bufs=1))
+        psum_t = ctx.enter_context(tc.psum_pool(name="psum_t", bufs=4))
+        psum_g = ctx.enter_context(tc.psum_pool(name="psum_g", bufs=2))
+        psum_b = ctx.enter_context(tc.psum_pool(name="psum_b", bufs=2))
+
+        x_sb = keep.tile([P, K], BF16)
+        nc.sync.dma_start(out=x_sb[:], in_=xt)
+        h_sb = keep.tile([P, K], BF16)
+        nc.sync.dma_start(out=h_sb[:], in_=hx)
+
+        b_rows = keep.tile([P, P], BF16)
+        nc.vector.memset(b_rows[:], 0.0)
+        for index, name in enumerate(gate_names):
+            nc.scalar.dma_start(
+                out=b_rows[ROWS * index : ROWS * (index + 1), :],
+                in_=gate_b[name].rearrange("(c j) -> c j", j=P),
+            )
+        cx_sb = keep.tile([P, H], BF16)
+        nc.scalar.dma_start(out=cx_sb[:], in_=cx)
+
+        weights_sb = {}
+        for name in gate_names:
+            for kind, source in (("w", gate_w[name]), ("r", gate_r[name])):
+                w_sb = keep.tile([P, ROWS * K], BF16, name="%s_%s_sb" % (kind, name))
+                nc.sync.dma_start(out=w_sb[:], in_=source.rearrange("(p r) k -> p (r k)", r=ROWS))
+                weights_sb[(kind, name)] = w_sb
+
+        ident_f32 = keep.tile([P, P], F32)
+        make_identity(nc, ident_f32[:])
+        ident_bf16 = keep.tile([P, P], BF16)
+        nc.vector.tensor_copy(out=ident_bf16[:], in_=ident_f32[:])
+        warm_in = keep.tile([P, 1], F32)
+        nc.vector.memset(warm_in[:], 0.0)
+        warm_out = keep.tile([P, 1], F32)
+        nc.scalar.activation(out=warm_out[:], in_=warm_in[:], func=ACT.Sigmoid)
+
+        def transpose_words(bank, slot, u, source_sb, first_word):
+            nc.tensor.transpose(
+                bank[:, slot, u, :],
+                source_sb[:].bitcast(F32)[:, first_word : first_word + P],
+                ident_f32[:],
+            )
+
+        xh_bank = psum_t.tile([P, 2, HALVES, P], F32, tag="bank")
+        for s, source_sb in enumerate((x_sb, h_sb)):
+            for u in range(HALVES):
+                transpose_words(xh_bank, s, u, source_sb, u * P)
+        xh_grouped = keep.tile([P, 2 * P * 4], BF16, align_bytes=64)
+        nc.vector.tensor_copy(
+            out=xh_grouped[:].bitcast(F32).rearrange("p (s n u) -> p s n u", s=2, u=HALVES),
+            in_=xh_bank[:].rearrange("p s u n -> p s n u"),
+        )
+        xh_codes = keep.tile([P, 2 * P], U32, align_bytes=64)
+        xh_scales = keep.tile([P, 2 * P], U8, align_bytes=64)
+        nc.vector.quantize_mx(out=xh_codes[:].bitcast(FP8X4), scales=xh_scales[:], in_=xh_grouped[:])
+        batch_cols = {"w": slice(0, P), "r": slice(P, 2 * P)}
+
+        b_cols_ps = psum_b.tile([P, P], BF16, tag="bias")
+        nc.tensor.transpose(b_cols_ps[:], b_rows[:], ident_bf16[:])
+        b_cols = keep.tile([P, GATES * ROWS], BF16)
+        nc.vector.tensor_copy(out=b_cols[:], in_=b_cols_ps[:, 0 : GATES * ROWS])
+        bias_all = keep.tile([P, GATES * H], BF16)
+        chunks_in_bank = 8
+        for half in range(2):
+            b_bank = psum_b.tile([P, chunks_in_bank * P], BF16, tag="bias")
+            for c in range(chunks_in_bank):
+                col = half * chunks_in_bank + c
+                nc.tensor.transpose(
+                    b_bank[:, c * P : (c + 1) * P],
+                    b_cols[:, col : col + 1].to_broadcast([P, P]),
+                    ident_bf16[:],
+                )
+            width = chunks_in_bank * P
+            nc.vector.tensor_copy(out=bias_all[:, half * width : (half + 1) * width], in_=b_bank[:])
+
+        acts = {}
+        for index, name in enumerate(gate_names):
+            gate_ps = psum_g.tile([P, H], F32, tag="gate")
+            for kind in ("w", "r"):
+                w_sb = weights_sb[(kind, name)]
+                grouped = stage.tile([P, H * 4], BF16, align_bytes=64, tag="grouped")
+                grouped_words = grouped[:].bitcast(F32).rearrange(
+                    "p (r n u) -> p r n u", r=ROWS, u=HALVES
+                )
+                for j in range(2):
+                    bank = psum_t.tile([P, 2, HALVES, P], F32, tag="bank")
+                    for s in range(2):
+                        for u in range(HALVES):
+                            transpose_words(bank, s, u, w_sb, (2 * j + s) * (K // 2) + u * P)
+                    nc.scalar.copy(
+                        out=grouped_words[:, 2 * j : 2 * j + 2, :, :],
+                        in_=bank[:].rearrange("p s u n -> p s n u"),
+                    )
+                codes = keep.tile([P, H], U32, align_bytes=64, name="codes_%s_%s" % (kind, name))
+                scales = keep.tile([P, H], U8, align_bytes=64, name="scales_%s_%s" % (kind, name))
+                nc.vector.quantize_mx(out=codes[:].bitcast(FP8X4), scales=scales[:], in_=grouped[:])
+                nc.tensor.matmul_mx(
+                    out=gate_ps[:],
+                    lhsT=xh_codes[:, batch_cols[kind]].bitcast(FP8X4),
+                    lhsT_scale=xh_scales[:, batch_cols[kind]],
+                    rhs=codes[:].bitcast(FP8X4),
+                    rhs_scale=scales[:],
+                    start=(kind == "w"),
+                    stop=(kind == "r"),
+                )
+            pre = work.tile([P, H], F32, name="pre_%s" % name)
+            nc.vector.tensor_tensor(
+                out=pre[:].rearrange("b (n r) -> b n r", r=ROWS),
+                in0=gate_ps[:].rearrange("b (r n) -> b n r", r=ROWS),
+                in1=bias_all[:, index * H : (index + 1) * H].rearrange("b (n r) -> b n r", r=ROWS),
+                op=ALU.add,
+            )
+            act = work.tile([P, H], F32, name="act_%s" % name)
+            nc.scalar.activation(out=act[:], in_=pre[:], func=gate_func[name])
+            acts[name] = act
+
+            if name == "f":
+                kept = work.tile([P, H], F32)
+                nc.vector.tensor_tensor(out=kept[:], in0=acts["f"][:], in1=cx_sb[:], op=ALU.mult)
+            if name == "g":
+                fresh = work.tile([P, H], F32)
+                nc.vector.tensor_tensor(out=fresh[:], in0=acts["i"][:], in1=acts["g"][:], op=ALU.mult)
+                ct = work.tile([P, H], F32)
+                nc.vector.tensor_tensor(out=ct[:], in0=kept[:], in1=fresh[:], op=ALU.add)
+                nc.sync.dma_start(out=out_1, in_=ct[:])
+                tanh_ct = work.tile([P, H], F32)
+                nc.scalar.activation(out=tanh_ct[:], in_=ct[:], func=ACT.Tanh)
+            if name == "o":
+                ht = work.tile([P, H], F32)
+                nc.vector.tensor_tensor(out=ht[:], in0=acts["o"][:], in1=tanh_ct[:], op=ALU.mult)
+                nc.sync.dma_start(out=out_0, in_=ht[:])

@@ -17,6 +17,7 @@ H = 512
 ROWS = 4
 HALVES = 2
 GATES = 4
+WARM_PASSES = 3
 
 FLOPS = 2 * P * (K + K) * GATES * H
 
@@ -31,42 +32,66 @@ def tile_lstmcell_s_kernel(
     gate_b = {"f": b_fg, "i": b_ig, "g": b_ci, "o": b_og}
     gate_func = {"f": ACT.Sigmoid, "i": ACT.Sigmoid, "g": ACT.Tanh, "o": ACT.Sigmoid}
 
+    matrices = []
+    for name in gate_names:
+        matrices.append(("w", name, gate_w[name]))
+        matrices.append(("r", name, gate_r[name]))
+    n_matrices = len(matrices)
+
     with ExitStack() as ctx:
         keep = ctx.enter_context(tc.tile_pool(name="keep", bufs=1))
         stage = ctx.enter_context(tc.tile_pool(name="stage", bufs=3))
-        work = ctx.enter_context(tc.tile_pool(name="work", bufs=1))
-        psum_t = ctx.enter_context(tc.psum_pool(name="psum_t", bufs=4))
+        psum_t = ctx.enter_context(tc.psum_pool(name="psum_t", bufs=5))
         psum_g = ctx.enter_context(tc.psum_pool(name="psum_g", bufs=2))
-        psum_b = ctx.enter_context(tc.psum_pool(name="psum_b", bufs=2))
+        psum_i = ctx.enter_context(tc.psum_pool(name="psum_i", bufs=1))
+        ctx.enter_context(tc.manual_schedule())
 
         x_sb = keep.tile([P, K], BF16)
         nc.sync.dma_start(out=x_sb[:], in_=xt)
         h_sb = keep.tile([P, K], BF16)
         nc.sync.dma_start(out=h_sb[:], in_=hx)
 
-        b_rows = keep.tile([P, P], BF16)
+        warm_in = keep.tile([P, 1], F32)
+        nc.vector.memset(warm_in[:], 0.0)
+        b_rows = keep.tile([P, 2 * P], BF16)
         nc.vector.memset(b_rows[:], 0.0)
         for index, name in enumerate(gate_names):
             nc.scalar.dma_start(
-                out=b_rows[ROWS * index : ROWS * (index + 1), :],
-                in_=gate_b[name].rearrange("(c j) -> c j", j=P),
+                out=b_rows[2 * index : 2 * (index + 1), :],
+                in_=gate_b[name].rearrange("(c j) -> c j", j=2 * P),
             )
+        idle_values = keep.tile([P, H * 4], BF16, align_bytes=64)
+        nc.vector.memset(idle_values[:], 0.0)
+        idle_codes = keep.tile([P, H], U32, align_bytes=64)
+        idle_scales = keep.tile([P, H], U8, align_bytes=64)
+        nc.vector.quantize_mx(out=idle_codes[:].bitcast(FP8X4), scales=idle_scales[:], in_=idle_values[:])
+        idle_ps = psum_i.tile([P, H], F32)
+
+        def idle_passes(count):
+            for i in range(count):
+                nc.tensor.matmul_mx(
+                    out=idle_ps[:],
+                    lhsT=idle_codes[:, 0:P].bitcast(FP8X4),
+                    lhsT_scale=idle_scales[:, 0:P],
+                    rhs=idle_codes[:].bitcast(FP8X4),
+                    rhs_scale=idle_scales[:],
+                    start=True,
+                    stop=True,
+                )
+
+        idle_passes(WARM_PASSES)
+
         cx_sb = keep.tile([P, H], BF16)
         nc.scalar.dma_start(out=cx_sb[:], in_=cx)
 
-        weights_sb = {}
-        for name in gate_names:
-            for kind, source in (("w", gate_w[name]), ("r", gate_r[name])):
-                w_sb = keep.tile([P, ROWS * K], BF16, name="%s_%s_sb" % (kind, name))
-                nc.sync.dma_start(out=w_sb[:], in_=source.rearrange("(p r) k -> p (r k)", r=ROWS))
-                weights_sb[(kind, name)] = w_sb
+        weights_sb = []
+        for kind, name, source in matrices:
+            w_sb = keep.tile([P, ROWS * K], BF16, name="%s_%s_sb" % (kind, name))
+            nc.sync.dma_start(out=w_sb[:], in_=source.rearrange("(p r) k -> p (r k)", r=ROWS))
+            weights_sb.append(w_sb)
 
         ident_f32 = keep.tile([P, P], F32)
         make_identity(nc, ident_f32[:])
-        ident_bf16 = keep.tile([P, P], BF16)
-        nc.vector.tensor_copy(out=ident_bf16[:], in_=ident_f32[:])
-        warm_in = keep.tile([P, 1], F32)
-        nc.vector.memset(warm_in[:], 0.0)
         warm_out = keep.tile([P, 1], F32)
         nc.scalar.activation(out=warm_out[:], in_=warm_in[:], func=ACT.Sigmoid)
 
@@ -86,82 +111,139 @@ def tile_lstmcell_s_kernel(
             out=xh_grouped[:].bitcast(F32).rearrange("p (s n u) -> p s n u", s=2, u=HALVES),
             in_=xh_bank[:].rearrange("p s u n -> p s n u"),
         )
+        b_cols_ps = psum_t.tile([P, P], F32, tag="bank")
+        nc.tensor.transpose(b_cols_ps[:], b_rows[:].bitcast(F32), ident_f32[:])
+        b_cols = keep.tile([P, 2 * GATES], F32)
+        nc.vector.tensor_copy(out=b_cols[:], in_=b_cols_ps[:, 0 : 2 * GATES])
+
         xh_codes = keep.tile([P, 2 * P], U32, align_bytes=64)
         xh_scales = keep.tile([P, 2 * P], U8, align_bytes=64)
         nc.vector.quantize_mx(out=xh_codes[:].bitcast(FP8X4), scales=xh_scales[:], in_=xh_grouped[:])
         batch_cols = {"w": slice(0, P), "r": slice(P, 2 * P)}
 
-        b_cols_ps = psum_b.tile([P, P], BF16, tag="bias")
-        nc.tensor.transpose(b_cols_ps[:], b_rows[:], ident_bf16[:])
-        b_cols = keep.tile([P, GATES * ROWS], BF16)
-        nc.vector.tensor_copy(out=b_cols[:], in_=b_cols_ps[:, 0 : GATES * ROWS])
         bias_all = keep.tile([P, GATES * H], BF16)
-        chunks_in_bank = 8
-        for half in range(2):
-            b_bank = psum_b.tile([P, chunks_in_bank * P], BF16, tag="bias")
-            for c in range(chunks_in_bank):
-                col = half * chunks_in_bank + c
-                nc.tensor.transpose(
-                    b_bank[:, c * P : (c + 1) * P],
-                    b_cols[:, col : col + 1].to_broadcast([P, P]),
-                    ident_bf16[:],
-                )
-            width = chunks_in_bank * P
-            nc.vector.tensor_copy(out=bias_all[:, half * width : (half + 1) * width], in_=b_bank[:])
 
+        grouped_tiles = {}
+        codes_tiles = {}
+        scales_tiles = {}
+        gate_banks = {}
+        pres = {}
         acts = {}
-        for index, name in enumerate(gate_names):
-            gate_ps = psum_g.tile([P, H], F32, tag="gate")
-            for kind in ("w", "r"):
-                w_sb = weights_sb[(kind, name)]
-                grouped = stage.tile([P, H * 4], BF16, align_bytes=64, tag="grouped")
-                grouped_words = grouped[:].bitcast(F32).rearrange(
-                    "p (r n u) -> p r n u", r=ROWS, u=HALVES
+        parts = {}
+
+        def transpose_and_copy(m):
+            grouped = stage.tile([P, H * 4], BF16, align_bytes=64, tag="grouped")
+            grouped_words = grouped[:].bitcast(F32).rearrange("p (r n u) -> p r n u", r=ROWS, u=HALVES)
+            for j in range(2):
+                bank = psum_t.tile([P, 2, HALVES, P], F32, tag="bank")
+                for s in range(2):
+                    for u in range(HALVES):
+                        transpose_words(bank, s, u, weights_sb[m], (2 * j + s) * (K // 2) + u * P)
+                if j == 1 and m == n_matrices - 1:
+                    copy_out = nc.vector.tensor_copy
+                else:
+                    copy_out = nc.scalar.copy
+                copy_out(
+                    out=grouped_words[:, 2 * j : 2 * j + 2, :, :],
+                    in_=bank[:].rearrange("p s u n -> p s n u"),
                 )
-                for j in range(2):
-                    bank = psum_t.tile([P, 2, HALVES, P], F32, tag="bank")
-                    for s in range(2):
-                        for u in range(HALVES):
-                            transpose_words(bank, s, u, w_sb, (2 * j + s) * (K // 2) + u * P)
-                    nc.scalar.copy(
-                        out=grouped_words[:, 2 * j : 2 * j + 2, :, :],
-                        in_=bank[:].rearrange("p s u n -> p s n u"),
-                    )
-                codes = keep.tile([P, H], U32, align_bytes=64, name="codes_%s_%s" % (kind, name))
-                scales = keep.tile([P, H], U8, align_bytes=64, name="scales_%s_%s" % (kind, name))
-                nc.vector.quantize_mx(out=codes[:].bitcast(FP8X4), scales=scales[:], in_=grouped[:])
-                nc.tensor.matmul_mx(
-                    out=gate_ps[:],
-                    lhsT=xh_codes[:, batch_cols[kind]].bitcast(FP8X4),
-                    lhsT_scale=xh_scales[:, batch_cols[kind]],
-                    rhs=codes[:].bitcast(FP8X4),
-                    rhs_scale=scales[:],
-                    start=(kind == "w"),
-                    stop=(kind == "r"),
-                )
-            pre = work.tile([P, H], F32, name="pre_%s" % name)
+            grouped_tiles[m] = grouped
+
+        def quantise(m):
+            codes = keep.tile([P, H], U32, align_bytes=64, name="codes_%d" % m)
+            scales = keep.tile([P, H], U8, align_bytes=64, name="scales_%d" % m)
+            nc.vector.quantize_mx(out=codes[:].bitcast(FP8X4), scales=scales[:], in_=grouped_tiles[m][:])
+            codes_tiles[m] = codes
+            scales_tiles[m] = scales
+
+        def multiply(m):
+            kind, name = matrices[m][0], matrices[m][1]
+            if kind == "w":
+                gate_banks[name] = psum_g.tile([P, H], F32, tag="gate", name="gate_%s" % name)
+            nc.tensor.matmul_mx(
+                out=gate_banks[name][:],
+                lhsT=xh_codes[:, batch_cols[kind]].bitcast(FP8X4),
+                lhsT_scale=xh_scales[:, batch_cols[kind]],
+                rhs=codes_tiles[m][:].bitcast(FP8X4),
+                rhs_scale=scales_tiles[m][:],
+                start=(kind == "w"),
+                stop=(kind == "r"),
+            )
+
+        def add_bias(index):
+            name = gate_names[index]
+            gate_ps = gate_banks[name]
+            pre = keep.tile([P, H], F32, name="pre_%s" % name)
             nc.vector.tensor_tensor(
                 out=pre[:].rearrange("b (n r) -> b n r", r=ROWS),
                 in0=gate_ps[:].rearrange("b (r n) -> b n r", r=ROWS),
                 in1=bias_all[:, index * H : (index + 1) * H].rearrange("b (n r) -> b n r", r=ROWS),
                 op=ALU.add,
             )
-            act = work.tile([P, H], F32, name="act_%s" % name)
-            nc.scalar.activation(out=act[:], in_=pre[:], func=gate_func[name])
+            pres[name] = pre
+
+        def activate(index):
+            name = gate_names[index]
+            act = keep.tile([P, H], F32, name="act_%s" % name)
+            nc.scalar.activation(out=act[:], in_=pres[name][:], func=gate_func[name])
             acts[name] = act
 
+        def gate_products(index):
+            name = gate_names[index]
             if name == "f":
-                kept = work.tile([P, H], F32)
+                kept = keep.tile([P, H], F32)
                 nc.vector.tensor_tensor(out=kept[:], in0=acts["f"][:], in1=cx_sb[:], op=ALU.mult)
+                parts["kept"] = kept
             if name == "g":
-                fresh = work.tile([P, H], F32)
+                fresh = keep.tile([P, H], F32)
                 nc.vector.tensor_tensor(out=fresh[:], in0=acts["i"][:], in1=acts["g"][:], op=ALU.mult)
-                ct = work.tile([P, H], F32)
-                nc.vector.tensor_tensor(out=ct[:], in0=kept[:], in1=fresh[:], op=ALU.add)
+                ct = keep.tile([P, H], F32)
+                nc.vector.tensor_tensor(out=ct[:], in0=parts["kept"][:], in1=fresh[:], op=ALU.add)
                 nc.sync.dma_start(out=out_1, in_=ct[:])
-                tanh_ct = work.tile([P, H], F32)
+                tanh_ct = keep.tile([P, H], F32)
                 nc.scalar.activation(out=tanh_ct[:], in_=ct[:], func=ACT.Tanh)
+                parts["tanh_ct"] = tanh_ct
             if name == "o":
-                ht = work.tile([P, H], F32)
-                nc.vector.tensor_tensor(out=ht[:], in0=acts["o"][:], in1=tanh_ct[:], op=ALU.mult)
+                ht = keep.tile([P, H], F32)
+                nc.vector.tensor_tensor(out=ht[:], in0=acts["o"][:], in1=parts["tanh_ct"][:], op=ALU.mult)
                 nc.sync.dma_start(out=out_0, in_=ht[:])
+
+        def spread_biases():
+            rows_in_bank = 4
+            for half in range(2):
+                b_bank = psum_t.tile([P, rows_in_bank * P], F32, tag="bank")
+                for c in range(rows_in_bank):
+                    col = half * rows_in_bank + c
+                    nc.tensor.transpose(
+                        b_bank[:, c * P : (c + 1) * P],
+                        b_cols[:, col : col + 1].to_broadcast([P, P]),
+                        ident_f32[:],
+                    )
+                width = rows_in_bank * P
+                nc.vector.tensor_copy(
+                    out=bias_all[:].bitcast(F32)[:, half * width : (half + 1) * width], in_=b_bank[:]
+                )
+
+        for m in range(n_matrices):
+            transpose_and_copy(m)
+            if m == 0:
+                spread_biases()
+            if m >= 1:
+                quantise(m - 1)
+            if m >= 2:
+                multiply(m - 2)
+            else:
+                idle_passes(1)
+            if m >= 3 and m % 2 == 1:
+                add_bias((m - 3) // 2)
+        quantise(n_matrices - 1)
+        activate(0)
+        activate(1)
+        activate(2)
+        gate_products(0)
+        multiply(n_matrices - 2)
+        multiply(n_matrices - 1)
+        gate_products(2)
+        add_bias(3)
+        activate(3)
+        gate_products(3)

@@ -14,10 +14,13 @@ ALU = mybir.AluOpType
 P = 128
 K = 512
 H = 512
+PACK = 4
 ROWS = 4
-HALVES = 2
+PLANES = 2
 GATES = 4
-WARM_PASSES = 3
+IDLE_COLS = 256
+WARM_PASSES = 8
+STEP_PASSES = 2
 
 FLOPS = 2 * P * (K + K) * GATES * H
 
@@ -31,7 +34,6 @@ def tile_lstmcell_s_kernel(
     gate_r = {"f": r_fg, "i": r_ig, "g": r_ci, "o": r_og}
     gate_b = {"f": b_fg, "i": b_ig, "g": b_ci, "o": b_og}
     gate_func = {"f": ACT.Sigmoid, "i": ACT.Sigmoid, "g": ACT.Tanh, "o": ACT.Sigmoid}
-
     matrices = []
     for name in gate_names:
         matrices.append(("w", name, gate_w[name]))
@@ -46,26 +48,40 @@ def tile_lstmcell_s_kernel(
         psum_i = ctx.enter_context(tc.psum_pool(name="psum_i", bufs=1))
         ctx.enter_context(tc.manual_schedule())
 
-        x_sb = keep.tile([P, K], BF16)
-        nc.sync.dma_start(out=x_sb[:], in_=xt)
-        h_sb = keep.tile([P, K], BF16)
-        nc.sync.dma_start(out=h_sb[:], in_=hx)
-
-        warm_in = keep.tile([P, 1], F32)
-        nc.vector.memset(warm_in[:], 0.0)
         b_rows = keep.tile([P, 2 * P], BF16)
-        nc.vector.memset(b_rows[:], 0.0)
+        nc.vector.memset(b_rows[:].bitcast(F32), 0.0)
         for index, name in enumerate(gate_names):
             nc.scalar.dma_start(
                 out=b_rows[2 * index : 2 * (index + 1), :],
                 in_=gate_b[name].rearrange("(c j) -> c j", j=2 * P),
             )
-        idle_values = keep.tile([P, H * 4], BF16, align_bytes=64)
-        nc.vector.memset(idle_values[:], 0.0)
-        idle_codes = keep.tile([P, H], U32, align_bytes=64)
-        idle_scales = keep.tile([P, H], U8, align_bytes=64)
+        cx_sb = keep.tile([P, H], BF16)
+        nc.scalar.dma_start(out=cx_sb[:], in_=cx)
+
+        weights_sb = []
+        for m, (kind, name, source) in enumerate(matrices):
+            w_sb = keep.tile([P, ROWS * K], BF16, name="%s_%s_sb" % (kind, name))
+            nc.sync.dma_start(out=w_sb[:], in_=source.rearrange("(p r) k -> p (r k)", r=ROWS))
+            weights_sb.append(w_sb)
+            if m == 1:
+                x_sb = keep.tile([P, K], BF16)
+                nc.sync.dma_start(out=x_sb[:], in_=xt)
+                h_sb = keep.tile([P, K], BF16)
+                nc.sync.dma_start(out=h_sb[:], in_=hx)
+
+        ident_f32 = keep.tile([P, P], F32)
+        make_identity(nc, ident_f32[:])
+        warm_in = keep.tile([P, 1], F32)
+        nc.vector.memset(warm_in[:], 0.0)
+        warm_out = keep.tile([P, 1], F32)
+        nc.scalar.activation(out=warm_out[:], in_=warm_in[:], func=ACT.Sigmoid)
+
+        idle_values = keep.tile([P, IDLE_COLS * PACK], BF16, align_bytes=64)
+        nc.vector.memset(idle_values[:].bitcast(F32), 0.0)
+        idle_codes = keep.tile([P, IDLE_COLS], U32, align_bytes=64)
+        idle_scales = keep.tile([P, IDLE_COLS], U8, align_bytes=64)
         nc.vector.quantize_mx(out=idle_codes[:].bitcast(FP8X4), scales=idle_scales[:], in_=idle_values[:])
-        idle_ps = psum_i.tile([P, H], F32)
+        idle_ps = psum_i.tile([P, IDLE_COLS], F32)
 
         def idle_passes(count):
             for i in range(count):
@@ -79,22 +95,6 @@ def tile_lstmcell_s_kernel(
                     stop=True,
                 )
 
-        idle_passes(WARM_PASSES)
-
-        cx_sb = keep.tile([P, H], BF16)
-        nc.scalar.dma_start(out=cx_sb[:], in_=cx)
-
-        weights_sb = []
-        for kind, name, source in matrices:
-            w_sb = keep.tile([P, ROWS * K], BF16, name="%s_%s_sb" % (kind, name))
-            nc.sync.dma_start(out=w_sb[:], in_=source.rearrange("(p r) k -> p (r k)", r=ROWS))
-            weights_sb.append(w_sb)
-
-        ident_f32 = keep.tile([P, P], F32)
-        make_identity(nc, ident_f32[:])
-        warm_out = keep.tile([P, 1], F32)
-        nc.scalar.activation(out=warm_out[:], in_=warm_in[:], func=ACT.Sigmoid)
-
         def transpose_words(bank, slot, u, source_sb, first_word):
             nc.tensor.transpose(
                 bank[:, slot, u, :],
@@ -102,26 +102,26 @@ def tile_lstmcell_s_kernel(
                 ident_f32[:],
             )
 
-        xh_bank = psum_t.tile([P, 2, HALVES, P], F32, tag="bank")
-        for s, source_sb in enumerate((x_sb, h_sb)):
-            for u in range(HALVES):
-                transpose_words(xh_bank, s, u, source_sb, u * P)
-        xh_grouped = keep.tile([P, 2 * P * 4], BF16, align_bytes=64)
-        nc.vector.tensor_copy(
-            out=xh_grouped[:].bitcast(F32).rearrange("p (s n u) -> p s n u", s=2, u=HALVES),
-            in_=xh_bank[:].rearrange("p s u n -> p s n u"),
-        )
+        idle_passes(WARM_PASSES)
         b_cols_ps = psum_t.tile([P, P], F32, tag="bank")
         nc.tensor.transpose(b_cols_ps[:], b_rows[:].bitcast(F32), ident_f32[:])
         b_cols = keep.tile([P, 2 * GATES], F32)
         nc.vector.tensor_copy(out=b_cols[:], in_=b_cols_ps[:, 0 : 2 * GATES])
-
-        xh_codes = keep.tile([P, 2 * P], U32, align_bytes=64)
-        xh_scales = keep.tile([P, 2 * P], U8, align_bytes=64)
-        nc.vector.quantize_mx(out=xh_codes[:].bitcast(FP8X4), scales=xh_scales[:], in_=xh_grouped[:])
-        batch_cols = {"w": slice(0, P), "r": slice(P, 2 * P)}
-
         bias_all = keep.tile([P, GATES * H], BF16)
+        rows_in_bank = 4
+        bank_words = rows_in_bank * P
+        for half in range(2):
+            b_bank = psum_t.tile([P, bank_words], F32, tag="bank")
+            for c in range(rows_in_bank):
+                col = half * rows_in_bank + c
+                nc.tensor.transpose(
+                    b_bank[:, c * P : (c + 1) * P],
+                    b_cols[:, col : col + 1].to_broadcast([P, P]),
+                    ident_f32[:],
+                )
+            nc.vector.tensor_copy(
+                out=bias_all[:].bitcast(F32)[:, half * bank_words : (half + 1) * bank_words], in_=b_bank[:]
+            )
 
         grouped_tiles = {}
         codes_tiles = {}
@@ -132,12 +132,12 @@ def tile_lstmcell_s_kernel(
         parts = {}
 
         def transpose_and_copy(m):
-            grouped = stage.tile([P, H * 4], BF16, align_bytes=64, tag="grouped")
-            grouped_words = grouped[:].bitcast(F32).rearrange("p (r n u) -> p r n u", r=ROWS, u=HALVES)
+            grouped = stage.tile([P, H * PACK], BF16, align_bytes=64, tag="grouped")
+            grouped_words = grouped[:].bitcast(F32).rearrange("p (r n u) -> p r n u", r=ROWS, u=PLANES)
             for j in range(2):
-                bank = psum_t.tile([P, 2, HALVES, P], F32, tag="bank")
+                bank = psum_t.tile([P, 2, PLANES, P], F32, tag="bank")
                 for s in range(2):
-                    for u in range(HALVES):
+                    for u in range(PLANES):
                         transpose_words(bank, s, u, weights_sb[m], (2 * j + s) * (K // 2) + u * P)
                 if j == 1 and m == n_matrices - 1:
                     copy_out = nc.vector.tensor_copy
@@ -156,6 +156,22 @@ def tile_lstmcell_s_kernel(
             codes_tiles[m] = codes
             scales_tiles[m] = scales
 
+        xh_codes = keep.tile([P, 2 * P], U32, align_bytes=64)
+        xh_scales = keep.tile([P, 2 * P], U8, align_bytes=64)
+        batch_cols = {"w": slice(0, P), "r": slice(P, 2 * P)}
+
+        def quantise_batch():
+            xh_bank = psum_t.tile([P, 2, PLANES, P], F32, tag="bank")
+            for s, source_sb in enumerate((x_sb, h_sb)):
+                for u in range(PLANES):
+                    transpose_words(xh_bank, s, u, source_sb, u * P)
+            xh_grouped = keep.tile([P, 2 * P * PACK], BF16, align_bytes=64)
+            nc.vector.tensor_copy(
+                out=xh_grouped[:].bitcast(F32).rearrange("p (s n u) -> p s n u", s=2, u=PLANES),
+                in_=xh_bank[:].rearrange("p s u n -> p s n u"),
+            )
+            nc.vector.quantize_mx(out=xh_codes[:].bitcast(FP8X4), scales=xh_scales[:], in_=xh_grouped[:])
+
         def multiply(m):
             kind, name = matrices[m][0], matrices[m][1]
             if kind == "w":
@@ -172,11 +188,10 @@ def tile_lstmcell_s_kernel(
 
         def add_bias(index):
             name = gate_names[index]
-            gate_ps = gate_banks[name]
             pre = keep.tile([P, H], F32, name="pre_%s" % name)
             nc.vector.tensor_tensor(
                 out=pre[:].rearrange("b (n r) -> b n r", r=ROWS),
-                in0=gate_ps[:].rearrange("b (r n) -> b n r", r=ROWS),
+                in0=gate_banks[name][:].rearrange("b (r n) -> b n r", r=ROWS),
                 in1=bias_all[:, index * H : (index + 1) * H].rearrange("b (n r) -> b n r", r=ROWS),
                 op=ALU.add,
             )
@@ -188,62 +203,46 @@ def tile_lstmcell_s_kernel(
             nc.scalar.activation(out=act[:], in_=pres[name][:], func=gate_func[name])
             acts[name] = act
 
-        def gate_products(index):
-            name = gate_names[index]
-            if name == "f":
-                kept = keep.tile([P, H], F32)
-                nc.vector.tensor_tensor(out=kept[:], in0=acts["f"][:], in1=cx_sb[:], op=ALU.mult)
-                parts["kept"] = kept
-            if name == "g":
-                fresh = keep.tile([P, H], F32)
-                nc.vector.tensor_tensor(out=fresh[:], in0=acts["i"][:], in1=acts["g"][:], op=ALU.mult)
-                ct = keep.tile([P, H], F32)
-                nc.vector.tensor_tensor(out=ct[:], in0=parts["kept"][:], in1=fresh[:], op=ALU.add)
-                nc.sync.dma_start(out=out_1, in_=ct[:])
-                tanh_ct = keep.tile([P, H], F32)
-                nc.scalar.activation(out=tanh_ct[:], in_=ct[:], func=ACT.Tanh)
-                parts["tanh_ct"] = tanh_ct
-            if name == "o":
-                ht = keep.tile([P, H], F32)
-                nc.vector.tensor_tensor(out=ht[:], in0=acts["o"][:], in1=parts["tanh_ct"][:], op=ALU.mult)
-                nc.sync.dma_start(out=out_0, in_=ht[:])
+        def keep_old_state():
+            kept = keep.tile([P, H], F32)
+            nc.vector.tensor_tensor(out=kept[:], in0=acts["f"][:], in1=cx_sb[:], op=ALU.mult)
+            parts["kept"] = kept
 
-        def spread_biases():
-            rows_in_bank = 4
-            for half in range(2):
-                b_bank = psum_t.tile([P, rows_in_bank * P], F32, tag="bank")
-                for c in range(rows_in_bank):
-                    col = half * rows_in_bank + c
-                    nc.tensor.transpose(
-                        b_bank[:, c * P : (c + 1) * P],
-                        b_cols[:, col : col + 1].to_broadcast([P, P]),
-                        ident_f32[:],
-                    )
-                width = rows_in_bank * P
-                nc.vector.tensor_copy(
-                    out=bias_all[:].bitcast(F32)[:, half * width : (half + 1) * width], in_=b_bank[:]
-                )
+        def new_state():
+            fresh = keep.tile([P, H], F32)
+            nc.vector.tensor_tensor(out=fresh[:], in0=acts["i"][:], in1=acts["g"][:], op=ALU.mult)
+            ct = keep.tile([P, H], F32)
+            nc.vector.tensor_tensor(out=ct[:], in0=parts["kept"][:], in1=fresh[:], op=ALU.add)
+            nc.sync.dma_start(out=out_1, in_=ct[:])
+            tanh_ct = keep.tile([P, H], F32)
+            nc.scalar.activation(out=tanh_ct[:], in_=ct[:], func=ACT.Tanh)
+            parts["tanh_ct"] = tanh_ct
+
+        def new_output():
+            ht = keep.tile([P, H], F32)
+            nc.vector.tensor_tensor(out=ht[:], in0=acts["o"][:], in1=parts["tanh_ct"][:], op=ALU.mult)
+            nc.sync.dma_start(out=out_0, in_=ht[:])
 
         for m in range(n_matrices):
             transpose_and_copy(m)
-            if m == 0:
-                spread_biases()
             if m >= 1:
                 quantise(m - 1)
+            if m == 1:
+                quantise_batch()
             if m >= 2:
                 multiply(m - 2)
             else:
-                idle_passes(1)
+                idle_passes(STEP_PASSES)
             if m >= 3 and m % 2 == 1:
                 add_bias((m - 3) // 2)
         quantise(n_matrices - 1)
         activate(0)
         activate(1)
         activate(2)
-        gate_products(0)
+        keep_old_state()
         multiply(n_matrices - 2)
         multiply(n_matrices - 1)
-        gate_products(2)
+        new_state()
         add_bias(3)
         activate(3)
-        gate_products(3)
+        new_output()

@@ -18,9 +18,7 @@ PACK = 4
 ROWS = 4
 PLANES = 2
 GATES = 4
-IDLE_COLS = 256
-WARM_PASSES = 8
-STEP_PASSES = 2
+WARM_PASSES = 3
 
 FLOPS = 2 * P * (K + K) * GATES * H
 
@@ -55,19 +53,18 @@ def tile_lstmcell_s_kernel(
                 out=b_rows[2 * index : 2 * (index + 1), :],
                 in_=gate_b[name].rearrange("(c j) -> c j", j=2 * P),
             )
-        cx_sb = keep.tile([P, H], BF16)
-        nc.scalar.dma_start(out=cx_sb[:], in_=cx)
-
+        x_sb = keep.tile([P, K], BF16)
+        nc.sync.dma_start(out=x_sb[:], in_=xt)
+        h_sb = keep.tile([P, K], BF16)
+        nc.sync.dma_start(out=h_sb[:], in_=hx)
         weights_sb = []
         for m, (kind, name, source) in enumerate(matrices):
             w_sb = keep.tile([P, ROWS * K], BF16, name="%s_%s_sb" % (kind, name))
             nc.sync.dma_start(out=w_sb[:], in_=source.rearrange("(p r) k -> p (r k)", r=ROWS))
             weights_sb.append(w_sb)
             if m == 1:
-                x_sb = keep.tile([P, K], BF16)
-                nc.sync.dma_start(out=x_sb[:], in_=xt)
-                h_sb = keep.tile([P, K], BF16)
-                nc.sync.dma_start(out=h_sb[:], in_=hx)
+                cx_sb = keep.tile([P, H], BF16)
+                nc.scalar.dma_start(out=cx_sb[:], in_=cx)
 
         ident_f32 = keep.tile([P, P], F32)
         make_identity(nc, ident_f32[:])
@@ -76,12 +73,12 @@ def tile_lstmcell_s_kernel(
         warm_out = keep.tile([P, 1], F32)
         nc.scalar.activation(out=warm_out[:], in_=warm_in[:], func=ACT.Sigmoid)
 
-        idle_values = keep.tile([P, IDLE_COLS * PACK], BF16, align_bytes=64)
+        idle_values = keep.tile([P, H * PACK], BF16, align_bytes=64)
         nc.vector.memset(idle_values[:].bitcast(F32), 0.0)
-        idle_codes = keep.tile([P, IDLE_COLS], U32, align_bytes=64)
-        idle_scales = keep.tile([P, IDLE_COLS], U8, align_bytes=64)
+        idle_codes = keep.tile([P, H], U32, align_bytes=64)
+        idle_scales = keep.tile([P, H], U8, align_bytes=64)
         nc.vector.quantize_mx(out=idle_codes[:].bitcast(FP8X4), scales=idle_scales[:], in_=idle_values[:])
-        idle_ps = psum_i.tile([P, IDLE_COLS], F32)
+        idle_ps = psum_i.tile([P, H], F32)
 
         def idle_passes(count):
             for i in range(count):
@@ -107,6 +104,17 @@ def tile_lstmcell_s_kernel(
         nc.tensor.transpose(b_cols_ps[:], b_rows[:].bitcast(F32), ident_f32[:])
         b_cols = keep.tile([P, 2 * GATES], F32)
         nc.vector.tensor_copy(out=b_cols[:], in_=b_cols_ps[:, 0 : 2 * GATES])
+
+        xh_bank = psum_t.tile([P, 2, PLANES, P], F32, tag="bank")
+        for s, source_sb in enumerate((x_sb, h_sb)):
+            for u in range(PLANES):
+                transpose_words(xh_bank, s, u, source_sb, u * P)
+        xh_grouped = keep.tile([P, 2 * P * PACK], BF16, align_bytes=64)
+        nc.vector.tensor_copy(
+            out=xh_grouped[:].bitcast(F32).rearrange("p (s n u) -> p s n u", s=2, u=PLANES),
+            in_=xh_bank[:].rearrange("p s u n -> p s n u"),
+        )
+
         bias_all = keep.tile([P, GATES * H], BF16)
         rows_in_bank = 4
         bank_words = rows_in_bank * P
@@ -123,13 +131,17 @@ def tile_lstmcell_s_kernel(
                 out=bias_all[:].bitcast(F32)[:, half * bank_words : (half + 1) * bank_words], in_=b_bank[:]
             )
 
+        xh_codes = keep.tile([P, 2 * P], U32, align_bytes=64)
+        xh_scales = keep.tile([P, 2 * P], U8, align_bytes=64)
+        nc.vector.quantize_mx(out=xh_codes[:].bitcast(FP8X4), scales=xh_scales[:], in_=xh_grouped[:])
+        batch_cols = {"w": slice(0, P), "r": slice(P, 2 * P)}
+
         grouped_tiles = {}
         codes_tiles = {}
         scales_tiles = {}
         gate_banks = {}
         pres = {}
         acts = {}
-        parts = {}
 
         def transpose_and_copy(m):
             grouped = stage.tile([P, H * PACK], BF16, align_bytes=64, tag="grouped")
@@ -156,22 +168,6 @@ def tile_lstmcell_s_kernel(
             codes_tiles[m] = codes
             scales_tiles[m] = scales
 
-        xh_codes = keep.tile([P, 2 * P], U32, align_bytes=64)
-        xh_scales = keep.tile([P, 2 * P], U8, align_bytes=64)
-        batch_cols = {"w": slice(0, P), "r": slice(P, 2 * P)}
-
-        def quantise_batch():
-            xh_bank = psum_t.tile([P, 2, PLANES, P], F32, tag="bank")
-            for s, source_sb in enumerate((x_sb, h_sb)):
-                for u in range(PLANES):
-                    transpose_words(xh_bank, s, u, source_sb, u * P)
-            xh_grouped = keep.tile([P, 2 * P * PACK], BF16, align_bytes=64)
-            nc.vector.tensor_copy(
-                out=xh_grouped[:].bitcast(F32).rearrange("p (s n u) -> p s n u", s=2, u=PLANES),
-                in_=xh_bank[:].rearrange("p s u n -> p s n u"),
-            )
-            nc.vector.quantize_mx(out=xh_codes[:].bitcast(FP8X4), scales=xh_scales[:], in_=xh_grouped[:])
-
         def multiply(m):
             kind, name = matrices[m][0], matrices[m][1]
             if kind == "w":
@@ -186,63 +182,61 @@ def tile_lstmcell_s_kernel(
                 stop=(kind == "r"),
             )
 
-        def add_bias(index):
+        whole = [(0, H)]
+        halves = [(0, H // 2), (H // 2, H)]
+        for name in gate_names:
+            pres[name] = keep.tile([P, H], F32, name="pre_%s" % name)
+            acts[name] = keep.tile([P, H], F32, name="act_%s" % name)
+        kept = keep.tile([P, H], F32)
+        fresh = keep.tile([P, H], F32)
+        ct = keep.tile([P, H], F32)
+        tanh_ct = keep.tile([P, H], F32)
+        ht = keep.tile([P, H], F32)
+
+        def add_bias(index, lo, hi):
             name = gate_names[index]
-            pre = keep.tile([P, H], F32, name="pre_%s" % name)
             nc.vector.tensor_tensor(
-                out=pre[:].rearrange("b (n r) -> b n r", r=ROWS),
-                in0=gate_banks[name][:].rearrange("b (r n) -> b n r", r=ROWS),
-                in1=bias_all[:, index * H : (index + 1) * H].rearrange("b (n r) -> b n r", r=ROWS),
+                out=pres[name][:, lo:hi].rearrange("b (n r) -> b n r", r=ROWS),
+                in0=gate_banks[name][:].rearrange("b (r n) -> b n r", r=ROWS)[:, lo // ROWS : hi // ROWS, :],
+                in1=bias_all[:, index * H + lo : index * H + hi].rearrange("b (n r) -> b n r", r=ROWS),
                 op=ALU.add,
             )
-            pres[name] = pre
 
-        def activate(index):
+        def activate(index, lo, hi):
             name = gate_names[index]
-            act = keep.tile([P, H], F32, name="act_%s" % name)
-            nc.scalar.activation(out=act[:], in_=pres[name][:], func=gate_func[name])
-            acts[name] = act
-
-        def keep_old_state():
-            kept = keep.tile([P, H], F32)
-            nc.vector.tensor_tensor(out=kept[:], in0=acts["f"][:], in1=cx_sb[:], op=ALU.mult)
-            parts["kept"] = kept
-
-        def new_state():
-            fresh = keep.tile([P, H], F32)
-            nc.vector.tensor_tensor(out=fresh[:], in0=acts["i"][:], in1=acts["g"][:], op=ALU.mult)
-            ct = keep.tile([P, H], F32)
-            nc.vector.tensor_tensor(out=ct[:], in0=parts["kept"][:], in1=fresh[:], op=ALU.add)
-            nc.sync.dma_start(out=out_1, in_=ct[:])
-            tanh_ct = keep.tile([P, H], F32)
-            nc.scalar.activation(out=tanh_ct[:], in_=ct[:], func=ACT.Tanh)
-            parts["tanh_ct"] = tanh_ct
-
-        def new_output():
-            ht = keep.tile([P, H], F32)
-            nc.vector.tensor_tensor(out=ht[:], in0=acts["o"][:], in1=parts["tanh_ct"][:], op=ALU.mult)
-            nc.sync.dma_start(out=out_0, in_=ht[:])
+            nc.scalar.activation(out=acts[name][:, lo:hi], in_=pres[name][:, lo:hi], func=gate_func[name])
 
         for m in range(n_matrices):
             transpose_and_copy(m)
+            if m >= 4 and m % 2 == 0:
+                for lo, hi in whole:
+                    activate((m - 4) // 2, lo, hi)
             if m >= 1:
                 quantise(m - 1)
-            if m == 1:
-                quantise_batch()
             if m >= 2:
                 multiply(m - 2)
             else:
-                idle_passes(STEP_PASSES)
-            if m >= 3 and m % 2 == 1:
-                add_bias((m - 3) // 2)
+                idle_passes(1)
+            if m == 3 or m == 5:
+                for lo, hi in whole:
+                    add_bias((m - 3) // 2, lo, hi)
+            if m == 5:
+                nc.vector.tensor_tensor(out=kept[:], in0=acts["f"][:], in1=cx_sb[:], op=ALU.mult)
+        for lo, hi in halves:
+            add_bias(2, lo, hi)
         quantise(n_matrices - 1)
-        activate(0)
-        activate(1)
-        activate(2)
-        keep_old_state()
+        for lo, hi in halves:
+            activate(2, lo, hi)
         multiply(n_matrices - 2)
         multiply(n_matrices - 1)
-        new_state()
-        add_bias(3)
-        activate(3)
-        new_output()
+        for lo, hi in halves:
+            nc.vector.tensor_tensor(out=fresh[:, lo:hi], in0=acts["i"][:, lo:hi], in1=acts["g"][:, lo:hi], op=ALU.mult)
+            nc.vector.tensor_tensor(out=ct[:, lo:hi], in0=kept[:, lo:hi], in1=fresh[:, lo:hi], op=ALU.add)
+            nc.scalar.activation(out=tanh_ct[:, lo:hi], in_=ct[:, lo:hi], func=ACT.Tanh)
+        nc.sync.dma_start(out=out_1, in_=ct[:])
+        for lo, hi in halves:
+            add_bias(3, lo, hi)
+            activate(3, lo, hi)
+        for lo, hi in halves:
+            nc.vector.tensor_tensor(out=ht[:, lo:hi], in0=acts["o"][:, lo:hi], in1=tanh_ct[:, lo:hi], op=ALU.mult)
+            nc.sync.dma_start(out=out_0[:, lo:hi], in_=ht[:, lo:hi])

@@ -213,10 +213,11 @@ def tile_lstmcell_s_kernel(
                     activate((m - 4) // 2, lo, hi)
             if m >= 1:
                 quantise(m - 1)
-            if m >= 2:
-                multiply(m - 2)
-            else:
+            if m < 2:
                 idle_passes(1)
+            elif m % 2 == 1:
+                multiply(m - 3)
+                multiply(m - 2)
             if m == 3 or m == 5:
                 for lo, hi in whole:
                     add_bias((m - 3) // 2, lo, hi)

@@ -18,7 +18,8 @@ PACK = 4
 ROWS = 4
 PLANES = 2
 GATES = 4
-WARM_PASSES = 3
+IDLE_N = 256
+WARM_PASSES = 6
 
 FLOPS = 2 * P * (K + K) * GATES * H
 
@@ -46,39 +47,45 @@ def tile_lstmcell_s_kernel(
         psum_i = ctx.enter_context(tc.psum_pool(name="psum_i", bufs=1))
         ctx.enter_context(tc.manual_schedule())
 
+        warm_in = keep.tile([P, 1], F32)
+        nc.gpsimd.memset(warm_in[:], 0.0)
+        warm_out = keep.tile([P, 1], F32)
+        nc.scalar.activation(out=warm_out[:], in_=warm_in[:], func=ACT.Sigmoid)
+        ident_f32 = keep.tile([P, P], F32)
+        make_identity(nc, ident_f32[:])
         b_rows = keep.tile([P, 2 * P], BF16)
         nc.vector.memset(b_rows[:].bitcast(F32), 0.0)
-        for index, name in enumerate(gate_names):
-            nc.scalar.dma_start(
-                out=b_rows[2 * index : 2 * (index + 1), :],
-                in_=gate_b[name].rearrange("(c j) -> c j", j=2 * P),
-            )
-        x_sb = keep.tile([P, K], BF16)
-        nc.sync.dma_start(out=x_sb[:], in_=xt)
-        h_sb = keep.tile([P, K], BF16)
-        nc.sync.dma_start(out=h_sb[:], in_=hx)
+        idle_values = keep.tile([P, IDLE_N * PACK], BF16, align_bytes=64)
+        nc.vector.memset(idle_values[:].bitcast(F32), 0.0)
+        idle_codes = keep.tile([P, IDLE_N], U32, align_bytes=64)
+        idle_scales = keep.tile([P, IDLE_N], U8, align_bytes=64)
+        nc.vector.quantize_mx(out=idle_codes[:].bitcast(FP8X4), scales=idle_scales[:], in_=idle_values[:])
+        idle_ps = psum_i.tile([P, IDLE_N], F32)
+
         weights_sb = []
         for m, (kind, name, source) in enumerate(matrices):
             w_sb = keep.tile([P, ROWS * K], BF16, name="%s_%s_sb" % (kind, name))
-            nc.sync.dma_start(out=w_sb[:], in_=source.rearrange("(p r) k -> p (r k)", r=ROWS))
             weights_sb.append(w_sb)
-            if m == 1:
+            if m == 0:
+                for j in range(2):
+                    nc.sync.dma_start(
+                        out=w_sb[:].rearrange("p (r k) -> p r k", r=ROWS)[:, 2 * j : 2 * j + 2, :],
+                        in_=source.rearrange("(p r) k -> p r k", r=ROWS)[:, 2 * j : 2 * j + 2, :],
+                    )
+                x_sb = keep.tile([P, K], BF16)
+                nc.sync.dma_start(out=x_sb[:], in_=xt)
+                h_sb = keep.tile([P, K], BF16)
+                nc.sync.dma_start(out=h_sb[:], in_=hx)
+                for index, gate in enumerate(gate_names):
+                    nc.sync.dma_start(
+                        out=b_rows[2 * index : 2 * (index + 1), :],
+                        in_=gate_b[gate].rearrange("(c j) -> c j", j=2 * P),
+                    )
+            else:
+                nc.sync.dma_start(out=w_sb[:], in_=source.rearrange("(p r) k -> p (r k)", r=ROWS))
+            if m == 3:
                 cx_sb = keep.tile([P, H], BF16)
-                nc.scalar.dma_start(out=cx_sb[:], in_=cx)
-
-        ident_f32 = keep.tile([P, P], F32)
-        make_identity(nc, ident_f32[:])
-        warm_in = keep.tile([P, 1], F32)
-        nc.vector.memset(warm_in[:], 0.0)
-        warm_out = keep.tile([P, 1], F32)
-        nc.scalar.activation(out=warm_out[:], in_=warm_in[:], func=ACT.Sigmoid)
-
-        idle_values = keep.tile([P, H * PACK], BF16, align_bytes=64)
-        nc.vector.memset(idle_values[:].bitcast(F32), 0.0)
-        idle_codes = keep.tile([P, H], U32, align_bytes=64)
-        idle_scales = keep.tile([P, H], U8, align_bytes=64)
-        nc.vector.quantize_mx(out=idle_codes[:].bitcast(FP8X4), scales=idle_scales[:], in_=idle_values[:])
-        idle_ps = psum_i.tile([P, H], F32)
+                nc.sync.dma_start(out=cx_sb[:], in_=cx)
 
         def idle_passes(count):
             for i in range(count):
@@ -99,42 +106,46 @@ def tile_lstmcell_s_kernel(
                 ident_f32[:],
             )
 
-        idle_passes(WARM_PASSES)
-        b_cols_ps = psum_t.tile([P, P], F32, tag="bank")
-        nc.tensor.transpose(b_cols_ps[:], b_rows[:].bitcast(F32), ident_f32[:])
         b_cols = keep.tile([P, 2 * GATES], F32)
-        nc.vector.tensor_copy(out=b_cols[:], in_=b_cols_ps[:, 0 : 2 * GATES])
-
-        xh_bank = psum_t.tile([P, 2, PLANES, P], F32, tag="bank")
-        for s, source_sb in enumerate((x_sb, h_sb)):
-            for u in range(PLANES):
-                transpose_words(xh_bank, s, u, source_sb, u * P)
-        xh_grouped = keep.tile([P, 2 * P * PACK], BF16, align_bytes=64)
-        nc.vector.tensor_copy(
-            out=xh_grouped[:].bitcast(F32).rearrange("p (s n u) -> p s n u", s=2, u=PLANES),
-            in_=xh_bank[:].rearrange("p s u n -> p s n u"),
-        )
-
         bias_all = keep.tile([P, GATES * H], BF16)
-        rows_in_bank = 4
-        bank_words = rows_in_bank * P
-        for half in range(2):
-            b_bank = psum_t.tile([P, bank_words], F32, tag="bank")
-            for c in range(rows_in_bank):
-                col = half * rows_in_bank + c
-                nc.tensor.transpose(
-                    b_bank[:, c * P : (c + 1) * P],
-                    b_cols[:, col : col + 1].to_broadcast([P, P]),
-                    ident_f32[:],
-                )
-            nc.vector.tensor_copy(
-                out=bias_all[:].bitcast(F32)[:, half * bank_words : (half + 1) * bank_words], in_=b_bank[:]
-            )
-
+        xh_grouped = keep.tile([P, 2 * P * PACK], BF16, align_bytes=64)
         xh_codes = keep.tile([P, 2 * P], U32, align_bytes=64)
         xh_scales = keep.tile([P, 2 * P], U8, align_bytes=64)
-        nc.vector.quantize_mx(out=xh_codes[:].bitcast(FP8X4), scales=xh_scales[:], in_=xh_grouped[:])
         batch_cols = {"w": slice(0, P), "r": slice(P, 2 * P)}
+
+        def bias_columns():
+            b_cols_ps = psum_t.tile([P, P], F32, tag="bank")
+            nc.tensor.transpose(b_cols_ps[:], b_rows[:].bitcast(F32), ident_f32[:])
+            nc.vector.tensor_copy(out=b_cols[:], in_=b_cols_ps[:, 0 : 2 * GATES])
+
+        def spread_bias():
+            rows_in_bank = 4
+            bank_words = rows_in_bank * P
+            for half in range(2):
+                b_bank = psum_t.tile([P, bank_words], F32, tag="bank")
+                for c in range(rows_in_bank):
+                    col = half * rows_in_bank + c
+                    nc.tensor.transpose(
+                        b_bank[:, c * P : (c + 1) * P],
+                        b_cols[:, col : col + 1].to_broadcast([P, P]),
+                        ident_f32[:],
+                    )
+                nc.vector.tensor_copy(
+                    out=bias_all[:].bitcast(F32)[:, half * bank_words : (half + 1) * bank_words], in_=b_bank[:]
+                )
+
+        def transpose_xh():
+            xh_bank = psum_t.tile([P, 2, PLANES, P], F32, tag="bank")
+            for s, source_sb in enumerate((x_sb, h_sb)):
+                for u in range(PLANES):
+                    transpose_words(xh_bank, s, u, source_sb, u * P)
+            nc.vector.tensor_copy(
+                out=xh_grouped[:].bitcast(F32).rearrange("p (s n u) -> p s n u", s=2, u=PLANES),
+                in_=xh_bank[:].rearrange("p s u n -> p s n u"),
+            )
+
+        def quantise_xh():
+            nc.vector.quantize_mx(out=xh_codes[:].bitcast(FP8X4), scales=xh_scales[:], in_=xh_grouped[:])
 
         grouped_tiles = {}
         codes_tiles = {}
@@ -206,15 +217,24 @@ def tile_lstmcell_s_kernel(
             name = gate_names[index]
             nc.scalar.activation(out=acts[name][:, lo:hi], in_=pres[name][:, lo:hi], func=gate_func[name])
 
+        idle_passes(WARM_PASSES)
         for m in range(n_matrices):
             transpose_and_copy(m)
+            if m == 0:
+                transpose_xh()
             if m >= 4 and m % 2 == 0:
                 for lo, hi in whole:
                     activate((m - 4) // 2, lo, hi)
+            if m == 1:
+                quantise_xh()
             if m >= 1:
                 quantise(m - 1)
+            if m == 1:
+                bias_columns()
+            if m == 2:
+                spread_bias()
             if m < 2:
-                idle_passes(1)
+                idle_passes(2)
             elif m % 2 == 1:
                 multiply(m - 3)
                 multiply(m - 2)

@@ -76,13 +76,14 @@ def tile_lstmcell_s_kernel(
                 nc.sync.dma_start(out=x_sb[:], in_=xt)
                 h_sb = keep.tile([P, K], BF16)
                 nc.sync.dma_start(out=h_sb[:], in_=hx)
+            else:
+                nc.sync.dma_start(out=w_sb[:], in_=source.rearrange("(p r) k -> p (r k)", r=ROWS))
+            if m == 2:
                 for index, gate in enumerate(gate_names):
                     nc.sync.dma_start(
                         out=b_rows[2 * index : 2 * (index + 1), :],
                         in_=gate_b[gate].rearrange("(c j) -> c j", j=2 * P),
                     )
-            else:
-                nc.sync.dma_start(out=w_sb[:], in_=source.rearrange("(p r) k -> p (r k)", r=ROWS))
             if m == 3:
                 cx_sb = keep.tile([P, H], BF16)
                 nc.sync.dma_start(out=cx_sb[:], in_=cx)
@@ -229,9 +230,9 @@ def tile_lstmcell_s_kernel(
                 quantise_xh()
             if m >= 1:
                 quantise(m - 1)
-            if m == 1:
-                bias_columns()
             if m == 2:
+                bias_columns()
+            if m == 3:
                 spread_bias()
             if m < 2:
                 idle_passes(2)

@@ -19,6 +19,7 @@ ROWS = 4
 PLANES = 2
 GATES = 4
 IDLE_N = 256
+TURNED = ("g", "o")
 WARM_PASSES = 6
 
 FLOPS = 2 * P * (K + K) * GATES * H
@@ -76,6 +77,14 @@ def tile_lstmcell_s_kernel(
                 nc.sync.dma_start(out=x_sb[:], in_=xt)
                 h_sb = keep.tile([P, K], BF16)
                 nc.sync.dma_start(out=h_sb[:], in_=hx)
+            elif name in TURNED:
+                w_halves = w_sb[:].rearrange("p (j c) -> p j c", j=2)
+                source_halves = source.rearrange("(j p s) k -> p j (s k)", j=2, s=2)
+                if m < n_matrices - 1:
+                    nc.sync.dma_start(out=w_halves, in_=source_halves)
+                else:
+                    for j in range(2):
+                        nc.sync.dma_start(out=w_halves[:, j, :], in_=source_halves[:, j, :])
             else:
                 nc.sync.dma_start(out=w_sb[:], in_=source.rearrange("(p r) k -> p (r k)", r=ROWS))
             if m == 2:
@@ -122,7 +131,7 @@ def tile_lstmcell_s_kernel(
         def spread_bias():
             rows_in_bank = 4
             bank_words = rows_in_bank * P
-            for half in range(2):
+            for half in range(1):
                 b_bank = psum_t.tile([P, bank_words], F32, tag="bank")
                 for c in range(rows_in_bank):
                     col = half * rows_in_bank + c
@@ -163,33 +172,32 @@ def tile_lstmcell_s_kernel(
                 for s in range(2):
                     for u in range(PLANES):
                         transpose_words(bank, s, u, weights_sb[m], (2 * j + s) * (K // 2) + u * P)
-                if j == 1 and m == n_matrices - 1:
-                    copy_out = nc.vector.tensor_copy
-                else:
-                    copy_out = nc.scalar.copy
-                copy_out(
+                nc.scalar.copy(
                     out=grouped_words[:, 2 * j : 2 * j + 2, :, :],
                     in_=bank[:].rearrange("p s u n -> p s n u"),
                 )
             grouped_tiles[m] = grouped
 
-        def quantise(m):
-            codes = keep.tile([P, H], U32, align_bytes=64, name="codes_%d" % m)
-            scales = keep.tile([P, H], U8, align_bytes=64, name="scales_%d" % m)
-            nc.vector.quantize_mx(out=codes[:].bitcast(FP8X4), scales=scales[:], in_=grouped_tiles[m][:])
-            codes_tiles[m] = codes
-            scales_tiles[m] = scales
+        def quantise(m, lo, hi):
+            if lo == 0:
+                codes_tiles[m] = keep.tile([P, H], U32, align_bytes=64, name="codes_%d" % m)
+                scales_tiles[m] = keep.tile([P, H], U8, align_bytes=64, name="scales_%d" % m)
+            nc.vector.quantize_mx(
+                out=codes_tiles[m][:, lo:hi].bitcast(FP8X4),
+                scales=scales_tiles[m][:, lo:hi],
+                in_=grouped_tiles[m][:, lo * PACK : hi * PACK],
+            )
 
-        def multiply(m):
+        def multiply(m, lo, hi):
             kind, name = matrices[m][0], matrices[m][1]
-            if kind == "w":
+            if kind == "w" and lo == 0:
                 gate_banks[name] = psum_g.tile([P, H], F32, tag="gate", name="gate_%s" % name)
             nc.tensor.matmul_mx(
-                out=gate_banks[name][:],
+                out=gate_banks[name][:, lo:hi],
                 lhsT=xh_codes[:, batch_cols[kind]].bitcast(FP8X4),
                 lhsT_scale=xh_scales[:, batch_cols[kind]],
-                rhs=codes_tiles[m][:].bitcast(FP8X4),
-                rhs_scale=scales_tiles[m][:],
+                rhs=codes_tiles[m][:, lo:hi].bitcast(FP8X4),
+                rhs_scale=scales_tiles[m][:, lo:hi],
                 start=(kind == "w"),
                 stop=(kind == "r"),
             )
@@ -214,6 +222,47 @@ def tile_lstmcell_s_kernel(
                 op=ALU.add,
             )
 
+        turned_banks = {}
+        turned_acts = {}
+        for name in TURNED:
+            turned_acts[name] = keep.tile([P, ROWS, P], F32, name="turned_%s" % name)
+
+        def multiply_turned(index, j):
+            name = gate_names[index]
+            turned_banks[name, j] = psum_g.tile([P, 2, P], F32, tag="gate", name="turned_%s%d" % (name, j))
+            for s in range(2):
+                c = 2 * j + s
+                for kind, m in (("w", 2 * index), ("r", 2 * index + 1)):
+                    nc.tensor.matmul_mx(
+                        out=turned_banks[name, j][:, s, :],
+                        lhsT=codes_tiles[m][:, c * P : (c + 1) * P].bitcast(FP8X4),
+                        lhsT_scale=scales_tiles[m][:, c * P : (c + 1) * P],
+                        rhs=xh_codes[:, batch_cols[kind]].bitcast(FP8X4),
+                        rhs_scale=xh_scales[:, batch_cols[kind]],
+                        start=(kind == "w"),
+                        stop=(kind == "r"),
+                    )
+
+        def activate_turned(index, j):
+            name = gate_names[index]
+            for s in range(2):
+                c = 2 * j + s
+                nc.scalar.activation(
+                    out=turned_acts[name][:, c, :],
+                    in_=turned_banks[name, j][:, s, :],
+                    func=gate_func[name],
+                    bias=b_cols[:].bitcast(BF16)[:, index * ROWS + c : index * ROWS + c + 1],
+                )
+
+        def turn_back(name, j):
+            bank = psum_t.tile([P, 2, P], F32, tag="bank")
+            for s in range(2):
+                nc.tensor.transpose(bank[:, s, :], turned_acts[name][:, 2 * j + s, :], ident_f32[:])
+            return bank[:].rearrange("b s n -> b n s")
+
+        def pairs(tile_half):
+            return tile_half.rearrange("b (n s) -> b n s", s=2)
+
         def activate(index, lo, hi):
             name = gate_names[index]
             nc.scalar.activation(out=acts[name][:, lo:hi], in_=pres[name][:, lo:hi], func=gate_func[name])
@@ -229,36 +278,40 @@ def tile_lstmcell_s_kernel(
             if m == 1:
                 quantise_xh()
             if m >= 1:
-                quantise(m - 1)
+                quantise(m - 1, 0, H)
             if m == 2:
                 bias_columns()
             if m == 3:
                 spread_bias()
             if m < 2:
                 idle_passes(2)
-            elif m % 2 == 1:
-                multiply(m - 3)
-                multiply(m - 2)
+            elif m == 3 or m == 5:
+                multiply(m - 3, 0, H)
+                multiply(m - 2, 0, H)
             if m == 3 or m == 5:
                 for lo, hi in whole:
                     add_bias((m - 3) // 2, lo, hi)
             if m == 5:
                 nc.vector.tensor_tensor(out=kept[:], in0=acts["f"][:], in1=cx_sb[:], op=ALU.mult)
+        for j in range(2):
+            multiply_turned(2, j)
+            activate_turned(2, j)
         for lo, hi in halves:
-            add_bias(2, lo, hi)
-        quantise(n_matrices - 1)
-        for lo, hi in halves:
-            activate(2, lo, hi)
-        multiply(n_matrices - 2)
-        multiply(n_matrices - 1)
-        for lo, hi in halves:
-            nc.vector.tensor_tensor(out=fresh[:, lo:hi], in0=acts["i"][:, lo:hi], in1=acts["g"][:, lo:hi], op=ALU.mult)
+            quantise(n_matrices - 1, lo, hi)
+        backs_g = []
+        for j in range(2):
+            backs_g.append(turn_back("g", j))
+        for j in range(2):
+            multiply_turned(3, j)
+        for j, (lo, hi) in enumerate(halves):
+            nc.vector.tensor_tensor(out=pairs(fresh[:, lo:hi]), in0=backs_g[j], in1=pairs(acts["i"][:, lo:hi]), op=ALU.mult)
             nc.vector.tensor_tensor(out=ct[:, lo:hi], in0=kept[:, lo:hi], in1=fresh[:, lo:hi], op=ALU.add)
+            activate_turned(3, j)
             nc.scalar.activation(out=tanh_ct[:, lo:hi], in_=ct[:, lo:hi], func=ACT.Tanh)
         nc.sync.dma_start(out=out_1, in_=ct[:])
-        for lo, hi in halves:
-            add_bias(3, lo, hi)
-            activate(3, lo, hi)
-        for lo, hi in halves:
-            nc.vector.tensor_tensor(out=ht[:, lo:hi], in0=acts["o"][:, lo:hi], in1=tanh_ct[:, lo:hi], op=ALU.mult)
+        backs_o = []
+        for j in range(2):
+            backs_o.append(turn_back("o", j))
+        for j, (lo, hi) in enumerate(halves):
+            nc.vector.tensor_tensor(out=pairs(ht[:, lo:hi]), in0=backs_o[j], in1=pairs(tanh_ct[:, lo:hi]), op=ALU.mult)
             nc.sync.dma_start(out=out_0[:, lo:hi], in_=ht[:, lo:hi])

@@ -42,10 +42,9 @@ def tile_lstmcell_s_kernel(
 
     with ExitStack() as ctx:
         keep = ctx.enter_context(tc.tile_pool(name="keep", bufs=1))
-        stage = ctx.enter_context(tc.tile_pool(name="stage", bufs=3))
-        psum_t = ctx.enter_context(tc.psum_pool(name="psum_t", bufs=5))
+        stage = ctx.enter_context(tc.tile_pool(name="stage", bufs=4))
+        psum_t = ctx.enter_context(tc.psum_pool(name="psum_t", bufs=6))
         psum_g = ctx.enter_context(tc.psum_pool(name="psum_g", bufs=2))
-        psum_i = ctx.enter_context(tc.psum_pool(name="psum_i", bufs=1))
         ctx.enter_context(tc.manual_schedule())
 
         warm_in = keep.tile([P, 1], F32)
@@ -54,14 +53,13 @@ def tile_lstmcell_s_kernel(
         nc.scalar.activation(out=warm_out[:], in_=warm_in[:], func=ACT.Sigmoid)
         ident_f32 = keep.tile([P, P], F32)
         make_identity(nc, ident_f32[:])
-        b_rows = keep.tile([P, 2 * P], BF16)
-        nc.vector.memset(b_rows[:].bitcast(F32), 0.0)
         idle_values = keep.tile([P, IDLE_N * PACK], BF16, align_bytes=64)
         nc.vector.memset(idle_values[:].bitcast(F32), 0.0)
         idle_codes = keep.tile([P, IDLE_N], U32, align_bytes=64)
         idle_scales = keep.tile([P, IDLE_N], U8, align_bytes=64)
         nc.vector.quantize_mx(out=idle_codes[:].bitcast(FP8X4), scales=idle_scales[:], in_=idle_values[:])
-        idle_ps = psum_i.tile([P, IDLE_N], F32)
+        b_rows = keep.tile([P, 2 * P], BF16)
+        nc.vector.memset(b_rows[:].bitcast(F32), 0.0)
 
         weights_sb = []
         for m, (kind, name, source) in enumerate(matrices):
@@ -83,11 +81,14 @@ def tile_lstmcell_s_kernel(
                 if m < n_matrices - 1:
                     nc.sync.dma_start(out=w_halves, in_=source_halves)
                 else:
-                    for j in range(2):
-                        nc.sync.dma_start(out=w_halves[:, j, :], in_=source_halves[:, j, :])
+                    nc.sync.dma_start(out=w_halves[:, 0, :], in_=source_halves[:, 0, :])
+                    for s in range(2):
+                        nc.sync.dma_start(
+                            out=w_halves[:, 1, s * K : (s + 1) * K], in_=source_halves[:, 1, s * K : (s + 1) * K]
+                        )
             else:
                 nc.sync.dma_start(out=w_sb[:], in_=source.rearrange("(p r) k -> p (r k)", r=ROWS))
-            if m == 2:
+            if m == 1:
                 for index, gate in enumerate(gate_names):
                     nc.sync.dma_start(
                         out=b_rows[2 * index : 2 * (index + 1), :],
@@ -97,10 +98,14 @@ def tile_lstmcell_s_kernel(
                 cx_sb = keep.tile([P, H], BF16)
                 nc.sync.dma_start(out=cx_sb[:], in_=cx)
 
+        gate_banks = {}
+        for name in ("f", "i"):
+            gate_banks[name] = psum_g.tile([P, H], F32, tag="gate", name="gate_%s" % name)
+
         def idle_passes(count):
             for i in range(count):
                 nc.tensor.matmul_mx(
-                    out=idle_ps[:],
+                    out=gate_banks["f"][:, 0:IDLE_N],
                     lhsT=idle_codes[:, 0:P].bitcast(FP8X4),
                     lhsT_scale=idle_scales[:, 0:P],
                     rhs=idle_codes[:].bitcast(FP8X4),
@@ -117,7 +122,8 @@ def tile_lstmcell_s_kernel(
             )
 
         b_cols = keep.tile([P, 2 * GATES], F32)
-        bias_all = keep.tile([P, GATES * H], BF16)
+        bias_words = 2 * P
+        bias_all = keep.tile([P, 2 * H], BF16)
         xh_grouped = keep.tile([P, 2 * P * PACK], BF16, align_bytes=64)
         xh_codes = keep.tile([P, 2 * P], U32, align_bytes=64)
         xh_scales = keep.tile([P, 2 * P], U8, align_bytes=64)
@@ -126,30 +132,24 @@ def tile_lstmcell_s_kernel(
         def bias_columns():
             b_cols_ps = psum_t.tile([P, P], F32, tag="bank")
             nc.tensor.transpose(b_cols_ps[:], b_rows[:].bitcast(F32), ident_f32[:])
-            nc.vector.tensor_copy(out=b_cols[:], in_=b_cols_ps[:, 0 : 2 * GATES])
+            nc.scalar.copy(out=b_cols[:], in_=b_cols_ps[:, 0 : 2 * GATES])
 
         def spread_bias():
-            rows_in_bank = 4
-            bank_words = rows_in_bank * P
-            for half in range(1):
-                b_bank = psum_t.tile([P, bank_words], F32, tag="bank")
-                for c in range(rows_in_bank):
-                    col = half * rows_in_bank + c
-                    nc.tensor.transpose(
-                        b_bank[:, c * P : (c + 1) * P],
-                        b_cols[:, col : col + 1].to_broadcast([P, P]),
-                        ident_f32[:],
-                    )
-                nc.vector.tensor_copy(
-                    out=bias_all[:].bitcast(F32)[:, half * bank_words : (half + 1) * bank_words], in_=b_bank[:]
+            b_bank = psum_t.tile([P, 2 * bias_words], F32, tag="bank")
+            for col in range(2 * bias_words // P):
+                nc.tensor.transpose(
+                    b_bank[:, col * P : (col + 1) * P],
+                    b_cols[:, col : col + 1].to_broadcast([P, P]),
+                    ident_f32[:],
                 )
+            nc.scalar.copy(out=bias_all[:].bitcast(F32), in_=b_bank[:])
 
         def transpose_xh():
             xh_bank = psum_t.tile([P, 2, PLANES, P], F32, tag="bank")
             for s, source_sb in enumerate((x_sb, h_sb)):
                 for u in range(PLANES):
                     transpose_words(xh_bank, s, u, source_sb, u * P)
-            nc.vector.tensor_copy(
+            nc.scalar.copy(
                 out=xh_grouped[:].bitcast(F32).rearrange("p (s n u) -> p s n u", s=2, u=PLANES),
                 in_=xh_bank[:].rearrange("p s u n -> p s n u"),
             )
@@ -160,51 +160,51 @@ def tile_lstmcell_s_kernel(
         grouped_tiles = {}
         codes_tiles = {}
         scales_tiles = {}
-        gate_banks = {}
         pres = {}
         acts = {}
+        banks = {}
 
-        def transpose_and_copy(m):
-            grouped = stage.tile([P, H * PACK], BF16, align_bytes=64, tag="grouped")
-            grouped_words = grouped[:].bitcast(F32).rearrange("p (r n u) -> p r n u", r=ROWS, u=PLANES)
-            for j in range(2):
-                bank = psum_t.tile([P, 2, PLANES, P], F32, tag="bank")
-                for s in range(2):
-                    for u in range(PLANES):
-                        transpose_words(bank, s, u, weights_sb[m], (2 * j + s) * (K // 2) + u * P)
-                nc.scalar.copy(
-                    out=grouped_words[:, 2 * j : 2 * j + 2, :, :],
-                    in_=bank[:].rearrange("p s u n -> p s n u"),
-                )
-            grouped_tiles[m] = grouped
+        def start_matrix(m):
+            grouped_tiles[m] = stage.tile([P, H * PACK], BF16, align_bytes=64, tag="grouped", name="grouped_%d" % m)
+            codes_tiles[m] = keep.tile([P, H], U32, align_bytes=64, name="codes_%d" % m)
+            scales_tiles[m] = keep.tile([P, H], U8, align_bytes=64, name="scales_%d" % m)
 
-        def quantise(m, lo, hi):
-            if lo == 0:
-                codes_tiles[m] = keep.tile([P, H], U32, align_bytes=64, name="codes_%d" % m)
-                scales_tiles[m] = keep.tile([P, H], U8, align_bytes=64, name="scales_%d" % m)
+        def transpose_rows(m, first, count):
+            bank = psum_t.tile([P, count, PLANES, P], F32, tag="bank", name="bank_%d_%d" % (m, first))
+            for s in range(count):
+                for u in range(PLANES):
+                    transpose_words(bank, s, u, weights_sb[m], (first + s) * (K // 2) + u * P)
+            banks[m, first] = bank
+
+        def copy_rows(m, first, count, copy):
+            words = grouped_tiles[m][:].bitcast(F32).rearrange("p (r n u) -> p r n u", r=ROWS, u=PLANES)
+            copy(
+                out=words[:, first : first + count, :, :],
+                in_=banks[m, first][:].rearrange("p s u n -> p s n u"),
+            )
+
+        def quantise_rows(m, first, count):
+            lo, hi = first * P, (first + count) * P
             nc.vector.quantize_mx(
                 out=codes_tiles[m][:, lo:hi].bitcast(FP8X4),
                 scales=scales_tiles[m][:, lo:hi],
                 in_=grouped_tiles[m][:, lo * PACK : hi * PACK],
             )
 
-        def multiply(m, lo, hi):
+        def multiply(m):
             kind, name = matrices[m][0], matrices[m][1]
-            if kind == "w" and lo == 0:
-                gate_banks[name] = psum_g.tile([P, H], F32, tag="gate", name="gate_%s" % name)
             nc.tensor.matmul_mx(
-                out=gate_banks[name][:, lo:hi],
+                out=gate_banks[name][:],
                 lhsT=xh_codes[:, batch_cols[kind]].bitcast(FP8X4),
                 lhsT_scale=xh_scales[:, batch_cols[kind]],
-                rhs=codes_tiles[m][:, lo:hi].bitcast(FP8X4),
-                rhs_scale=scales_tiles[m][:, lo:hi],
+                rhs=codes_tiles[m][:].bitcast(FP8X4),
+                rhs_scale=scales_tiles[m][:],
                 start=(kind == "w"),
                 stop=(kind == "r"),
             )
 
-        whole = [(0, H)]
         halves = [(0, H // 2), (H // 2, H)]
-        for name in gate_names:
+        for name in ("f", "i"):
             pres[name] = keep.tile([P, H], F32, name="pre_%s" % name)
             acts[name] = keep.tile([P, H], F32, name="act_%s" % name)
         kept = keep.tile([P, H], F32)
@@ -213,14 +213,18 @@ def tile_lstmcell_s_kernel(
         tanh_ct = keep.tile([P, H], F32)
         ht = keep.tile([P, H], F32)
 
-        def add_bias(index, lo, hi):
+        def add_bias(index):
             name = gate_names[index]
             nc.vector.tensor_tensor(
-                out=pres[name][:, lo:hi].rearrange("b (n r) -> b n r", r=ROWS),
-                in0=gate_banks[name][:].rearrange("b (r n) -> b n r", r=ROWS)[:, lo // ROWS : hi // ROWS, :],
-                in1=bias_all[:, index * H + lo : index * H + hi].rearrange("b (n r) -> b n r", r=ROWS),
+                out=pres[name][:].rearrange("b (n r) -> b n r", r=ROWS),
+                in0=gate_banks[name][:].rearrange("b (r n) -> b n r", r=ROWS),
+                in1=bias_all[:, index * H : (index + 1) * H].rearrange("b (n r) -> b n r", r=ROWS),
                 op=ALU.add,
             )
+
+        def activate(index):
+            name = gate_names[index]
+            nc.scalar.activation(out=acts[name][:], in_=pres[name][:], func=gate_func[name])
 
         turned_banks = {}
         turned_acts = {}
@@ -255,7 +259,7 @@ def tile_lstmcell_s_kernel(
                 )
 
         def turn_back(name, j):
-            bank = psum_t.tile([P, 2, P], F32, tag="bank")
+            bank = psum_t.tile([P, 2, P], F32, tag="bank", name="back_%s%d" % (name, j))
             for s in range(2):
                 nc.tensor.transpose(bank[:, s, :], turned_acts[name][:, 2 * j + s, :], ident_f32[:])
             return bank[:].rearrange("b s n -> b n s")
@@ -263,41 +267,49 @@ def tile_lstmcell_s_kernel(
         def pairs(tile_half):
             return tile_half.rearrange("b (n s) -> b n s", s=2)
 
-        def activate(index, lo, hi):
-            name = gate_names[index]
-            nc.scalar.activation(out=acts[name][:, lo:hi], in_=pres[name][:, lo:hi], func=gate_func[name])
-
         idle_passes(WARM_PASSES)
-        for m in range(n_matrices):
-            transpose_and_copy(m)
+        for m in range(n_matrices - 1):
+            start_matrix(m)
+            for first in (0, 2):
+                transpose_rows(m, first, 2)
+            copy_rows(m, 0, 2, nc.scalar.copy)
+            copy_rows(m, 2, 2, nc.vector.tensor_copy if m % 2 == 0 else nc.scalar.copy)
+            for first in (0, 2):
+                quantise_rows(m, first, 2)
             if m == 0:
                 transpose_xh()
-            if m >= 4 and m % 2 == 0:
-                for lo, hi in whole:
-                    activate((m - 4) // 2, lo, hi)
             if m == 1:
-                quantise_xh()
-            if m >= 1:
-                quantise(m - 1, 0, H)
-            if m == 2:
-                bias_columns()
-            if m == 3:
-                spread_bias()
-            if m < 2:
                 idle_passes(2)
-            elif m == 3 or m == 5:
-                multiply(m - 3, 0, H)
-                multiply(m - 2, 0, H)
-            if m == 3 or m == 5:
-                for lo, hi in whole:
-                    add_bias((m - 3) // 2, lo, hi)
+                bias_columns()
+                quantise_xh()
+            if m == 2:
+                spread_bias()
+            if m == 3:
+                multiply(0)
+                multiply(1)
+                add_bias(0)
             if m == 5:
-                nc.vector.tensor_tensor(out=kept[:], in0=acts["f"][:], in1=cx_sb[:], op=ALU.mult)
+                activate(0)
+                multiply(2)
+                multiply(3)
+                add_bias(1)
+        last = n_matrices - 1
+        start_matrix(last)
+        transpose_rows(last, 0, 2)
+        transpose_rows(last, 2, 1)
+        transpose_rows(last, 3, 1)
+        copy_rows(last, 0, 2, nc.scalar.copy)
         for j in range(2):
             multiply_turned(2, j)
+        copy_rows(last, 2, 1, nc.vector.tensor_copy)
+        copy_rows(last, 3, 1, nc.scalar.copy)
+        for j in range(2):
             activate_turned(2, j)
-        for lo, hi in halves:
-            quantise(n_matrices - 1, lo, hi)
+        quantise_rows(last, 0, 2)
+        quantise_rows(last, 2, 1)
+        quantise_rows(last, 3, 1)
+        nc.vector.tensor_tensor(out=kept[:], in0=acts["f"][:], in1=cx_sb[:], op=ALU.mult)
+        activate(1)
         backs_g = []
         for j in range(2):
             backs_g.append(turn_back("g", j))
@@ -305,8 +317,11 @@ def tile_lstmcell_s_kernel(
             multiply_turned(3, j)
         for j, (lo, hi) in enumerate(halves):
             nc.vector.tensor_tensor(out=pairs(fresh[:, lo:hi]), in0=backs_g[j], in1=pairs(acts["i"][:, lo:hi]), op=ALU.mult)
+        for j, (lo, hi) in enumerate(halves):
             nc.vector.tensor_tensor(out=ct[:, lo:hi], in0=kept[:, lo:hi], in1=fresh[:, lo:hi], op=ALU.add)
+        for j in range(2):
             activate_turned(3, j)
+        for j, (lo, hi) in enumerate(halves):
             nc.scalar.activation(out=tanh_ct[:, lo:hi], in_=ct[:, lo:hi], func=ACT.Tanh)
         nc.sync.dma_start(out=out_1, in_=ct[:])
         backs_o = []

@@ -19,7 +19,6 @@ ROWS = 4
 PLANES = 2
 GATES = 4
 IDLE_N = 256
-TURNED = ("g", "o")
 WARM_PASSES = 6
 
 FLOPS = 2 * P * (K + K) * GATES * H
@@ -58,10 +57,8 @@ def tile_lstmcell_s_kernel(
         idle_codes = keep.tile([P, IDLE_N], U32, align_bytes=64)
         idle_scales = keep.tile([P, IDLE_N], U8, align_bytes=64)
         nc.vector.quantize_mx(out=idle_codes[:].bitcast(FP8X4), scales=idle_scales[:], in_=idle_values[:])
-        b_rows = keep.tile([P, 2 * P], BF16)
-        nc.vector.memset(b_rows[:].bitcast(F32), 0.0)
-
         weights_sb = []
+        b_cols = {}
         for m, (kind, name, source) in enumerate(matrices):
             w_sb = keep.tile([P, ROWS * K], BF16, name="%s_%s_sb" % (kind, name))
             weights_sb.append(w_sb)
@@ -75,7 +72,7 @@ def tile_lstmcell_s_kernel(
                 nc.sync.dma_start(out=x_sb[:], in_=xt)
                 h_sb = keep.tile([P, K], BF16)
                 nc.sync.dma_start(out=h_sb[:], in_=hx)
-            elif name in TURNED:
+            elif name == "o":
                 w_halves = w_sb[:].rearrange("p (j c) -> p j c", j=2)
                 source_halves = source.rearrange("(j p s) k -> p j (s k)", j=2, s=2)
                 if m < n_matrices - 1:
@@ -88,24 +85,25 @@ def tile_lstmcell_s_kernel(
                         )
             else:
                 nc.sync.dma_start(out=w_sb[:], in_=source.rearrange("(p r) k -> p (r k)", r=ROWS))
-            if m == 1:
-                for index, gate in enumerate(gate_names):
-                    nc.sync.dma_start(
-                        out=b_rows[2 * index : 2 * (index + 1), :],
-                        in_=gate_b[gate].rearrange("(c j) -> c j", j=2 * P),
-                    )
-            if m == 3:
-                cx_sb = keep.tile([P, H], BF16)
-                nc.sync.dma_start(out=cx_sb[:], in_=cx)
+            if m == 2:
+                for gate in gate_names:
+                    b_cols[gate] = keep.tile([P, ROWS], BF16, name="b_%s" % gate)
+                    if gate == "o":
+                        nc.sync.dma_start(
+                            out=b_cols[gate][:].rearrange("p (j s) -> p j s", j=2),
+                            in_=gate_b[gate].rearrange("(j p s) -> p j s", j=2, s=2),
+                        )
+                    else:
+                        nc.sync.dma_start(out=b_cols[gate][:], in_=gate_b[gate].rearrange("(p r) -> p r", r=ROWS))
+        cx_sb = keep.tile([P, H], BF16)
+        nc.sync.dma_start(out=cx_sb[:], in_=cx)
 
-        gate_banks = {}
-        for name in ("f", "i"):
-            gate_banks[name] = psum_g.tile([P, H], F32, tag="gate", name="gate_%s" % name)
+        gate_banks = {"f": psum_g.tile([P, ROWS, P], F32, tag="gate", name="gate_f")}
 
         def idle_passes(count):
             for i in range(count):
                 nc.tensor.matmul_mx(
-                    out=gate_banks["f"][:, 0:IDLE_N],
+                    out=gate_banks["f"][:, 0 : IDLE_N // P, :].rearrange("p r n -> p (r n)"),
                     lhsT=idle_codes[:, 0:P].bitcast(FP8X4),
                     lhsT_scale=idle_scales[:, 0:P],
                     rhs=idle_codes[:].bitcast(FP8X4),
@@ -121,28 +119,10 @@ def tile_lstmcell_s_kernel(
                 ident_f32[:],
             )
 
-        b_cols = keep.tile([P, 2 * GATES], F32)
-        bias_words = 2 * P
-        bias_all = keep.tile([P, 2 * H], BF16)
         xh_grouped = keep.tile([P, 2 * P * PACK], BF16, align_bytes=64)
         xh_codes = keep.tile([P, 2 * P], U32, align_bytes=64)
         xh_scales = keep.tile([P, 2 * P], U8, align_bytes=64)
         batch_cols = {"w": slice(0, P), "r": slice(P, 2 * P)}
-
-        def bias_columns():
-            b_cols_ps = psum_t.tile([P, P], F32, tag="bank")
-            nc.tensor.transpose(b_cols_ps[:], b_rows[:].bitcast(F32), ident_f32[:])
-            nc.scalar.copy(out=b_cols[:], in_=b_cols_ps[:, 0 : 2 * GATES])
-
-        def spread_bias():
-            b_bank = psum_t.tile([P, 2 * bias_words], F32, tag="bank")
-            for col in range(2 * bias_words // P):
-                nc.tensor.transpose(
-                    b_bank[:, col * P : (col + 1) * P],
-                    b_cols[:, col : col + 1].to_broadcast([P, P]),
-                    ident_f32[:],
-                )
-            nc.scalar.copy(out=bias_all[:].bitcast(F32), in_=b_bank[:])
 
         def transpose_xh():
             xh_bank = psum_t.tile([P, 2, PLANES, P], F32, tag="bank")
@@ -160,7 +140,6 @@ def tile_lstmcell_s_kernel(
         grouped_tiles = {}
         codes_tiles = {}
         scales_tiles = {}
-        pres = {}
         acts = {}
         banks = {}
 
@@ -191,54 +170,23 @@ def tile_lstmcell_s_kernel(
                 in_=grouped_tiles[m][:, lo * PACK : hi * PACK],
             )
 
-        def multiply(m):
-            kind, name = matrices[m][0], matrices[m][1]
-            nc.tensor.matmul_mx(
-                out=gate_banks[name][:],
-                lhsT=xh_codes[:, batch_cols[kind]].bitcast(FP8X4),
-                lhsT_scale=xh_scales[:, batch_cols[kind]],
-                rhs=codes_tiles[m][:].bitcast(FP8X4),
-                rhs_scale=scales_tiles[m][:],
-                start=(kind == "w"),
-                stop=(kind == "r"),
-            )
-
         halves = [(0, H // 2), (H // 2, H)]
-        for name in ("f", "i"):
-            pres[name] = keep.tile([P, H], F32, name="pre_%s" % name)
-            acts[name] = keep.tile([P, H], F32, name="act_%s" % name)
+        for name in gate_names:
+            acts[name] = keep.tile([P, ROWS, P], F32, name="act_%s" % name)
+        product = keep.tile([P, ROWS, P], F32)
         kept = keep.tile([P, H], F32)
-        fresh = keep.tile([P, H], F32)
         ct = keep.tile([P, H], F32)
         tanh_ct = keep.tile([P, H], F32)
         ht = keep.tile([P, H], F32)
 
-        def add_bias(index):
+        def multiply(index, slots):
             name = gate_names[index]
-            nc.vector.tensor_tensor(
-                out=pres[name][:].rearrange("b (n r) -> b n r", r=ROWS),
-                in0=gate_banks[name][:].rearrange("b (r n) -> b n r", r=ROWS),
-                in1=bias_all[:, index * H : (index + 1) * H].rearrange("b (n r) -> b n r", r=ROWS),
-                op=ALU.add,
-            )
-
-        def activate(index):
-            name = gate_names[index]
-            nc.scalar.activation(out=acts[name][:], in_=pres[name][:], func=gate_func[name])
-
-        turned_banks = {}
-        turned_acts = {}
-        for name in TURNED:
-            turned_acts[name] = keep.tile([P, ROWS, P], F32, name="turned_%s" % name)
-
-        def multiply_turned(index, j):
-            name = gate_names[index]
-            turned_banks[name, j] = psum_g.tile([P, 2, P], F32, tag="gate", name="turned_%s%d" % (name, j))
-            for s in range(2):
-                c = 2 * j + s
+            if name not in gate_banks:
+                gate_banks[name] = psum_g.tile([P, ROWS, P], F32, tag="gate", name="gate_%s" % name)
+            for c in slots:
                 for kind, m in (("w", 2 * index), ("r", 2 * index + 1)):
                     nc.tensor.matmul_mx(
-                        out=turned_banks[name, j][:, s, :],
+                        out=gate_banks[name][:, c, :],
                         lhsT=codes_tiles[m][:, c * P : (c + 1) * P].bitcast(FP8X4),
                         lhsT_scale=scales_tiles[m][:, c * P : (c + 1) * P],
                         rhs=xh_codes[:, batch_cols[kind]].bitcast(FP8X4),
@@ -247,86 +195,92 @@ def tile_lstmcell_s_kernel(
                         stop=(kind == "r"),
                     )
 
-        def activate_turned(index, j):
+        def activate(index, slots):
             name = gate_names[index]
-            for s in range(2):
-                c = 2 * j + s
+            for c in slots:
                 nc.scalar.activation(
-                    out=turned_acts[name][:, c, :],
-                    in_=turned_banks[name, j][:, s, :],
+                    out=acts[name][:, c, :],
+                    in_=gate_banks[name][:, c, :],
                     func=gate_func[name],
-                    bias=b_cols[:].bitcast(BF16)[:, index * ROWS + c : index * ROWS + c + 1],
+                    bias=b_cols[name][:, c : c + 1],
                 )
 
-        def turn_back(name, j):
-            bank = psum_t.tile([P, 2, P], F32, tag="bank", name="back_%s%d" % (name, j))
-            for s in range(2):
-                nc.tensor.transpose(bank[:, s, :], turned_acts[name][:, 2 * j + s, :], ident_f32[:])
-            return bank[:].rearrange("b s n -> b n s")
+        def turn_back(source, slots, label):
+            bank = psum_t.tile([P, len(slots), P], F32, tag="bank", name="back_%s" % label)
+            for i, c in enumerate(slots):
+                nc.tensor.transpose(bank[:, i, :], source[:, c, :], ident_f32[:])
+            return bank
 
-        def pairs(tile_half):
-            return tile_half.rearrange("b (n s) -> b n s", s=2)
+        def units(tile_part, slots):
+            return tile_part.rearrange("b (n r) -> b n r", r=slots)
 
+        every = range(ROWS)
         idle_passes(WARM_PASSES)
         for m in range(n_matrices - 1):
             start_matrix(m)
             for first in (0, 2):
                 transpose_rows(m, first, 2)
             copy_rows(m, 0, 2, nc.scalar.copy)
-            copy_rows(m, 2, 2, nc.vector.tensor_copy if m % 2 == 0 else nc.scalar.copy)
+            copy_rows(m, 2, 2, nc.vector.tensor_copy if 0 < m < 6 else nc.scalar.copy)
             for first in (0, 2):
                 quantise_rows(m, first, 2)
             if m == 0:
                 transpose_xh()
-            if m == 1:
-                idle_passes(2)
-                bias_columns()
                 quantise_xh()
-            if m == 2:
-                spread_bias()
+            if m < 2:
+                idle_passes(2)
             if m == 3:
-                multiply(0)
-                multiply(1)
-                add_bias(0)
+                multiply(0, every)
+                activate(0, every)
             if m == 5:
-                activate(0)
-                multiply(2)
-                multiply(3)
-                add_bias(1)
+                multiply(1, every)
+                activate(1, every)
+        back_f = turn_back(acts["f"], every, "f")
         last = n_matrices - 1
         start_matrix(last)
         transpose_rows(last, 0, 2)
         transpose_rows(last, 2, 1)
         transpose_rows(last, 3, 1)
+        multiply(2, every)
         copy_rows(last, 0, 2, nc.scalar.copy)
-        for j in range(2):
-            multiply_turned(2, j)
         copy_rows(last, 2, 1, nc.vector.tensor_copy)
         copy_rows(last, 3, 1, nc.scalar.copy)
-        for j in range(2):
-            activate_turned(2, j)
+        activate(2, every)
         quantise_rows(last, 0, 2)
         quantise_rows(last, 2, 1)
         quantise_rows(last, 3, 1)
-        nc.vector.tensor_tensor(out=kept[:], in0=acts["f"][:], in1=cx_sb[:], op=ALU.mult)
-        activate(1)
-        backs_g = []
         for j in range(2):
-            backs_g.append(turn_back("g", j))
-        for j in range(2):
-            multiply_turned(3, j)
+            nc.vector.tensor_tensor(
+                out=product[:, 2 * j : 2 * j + 2, :],
+                in0=acts["i"][:, 2 * j : 2 * j + 2, :],
+                in1=acts["g"][:, 2 * j : 2 * j + 2, :],
+                op=ALU.mult,
+            )
+        nc.vector.tensor_tensor(
+            out=units(kept[:], ROWS), in0=back_f[:].rearrange("b r n -> b n r"), in1=units(cx_sb[:], ROWS), op=ALU.mult
+        )
+        multiply(3, (0, 1))
+        multiply(3, (2, 3))
+        back_p = turn_back(product, every, "p")
         for j, (lo, hi) in enumerate(halves):
-            nc.vector.tensor_tensor(out=pairs(fresh[:, lo:hi]), in0=backs_g[j], in1=pairs(acts["i"][:, lo:hi]), op=ALU.mult)
-        for j, (lo, hi) in enumerate(halves):
-            nc.vector.tensor_tensor(out=ct[:, lo:hi], in0=kept[:, lo:hi], in1=fresh[:, lo:hi], op=ALU.add)
-        for j in range(2):
-            activate_turned(3, j)
+            nc.vector.tensor_tensor(
+                out=units(ct[:, lo:hi], ROWS),
+                in0=back_p[:, :, lo // ROWS : hi // ROWS].rearrange("b r n -> b n r"),
+                in1=units(kept[:, lo:hi], ROWS),
+                op=ALU.add,
+            )
+        activate(3, every)
         for j, (lo, hi) in enumerate(halves):
             nc.scalar.activation(out=tanh_ct[:, lo:hi], in_=ct[:, lo:hi], func=ACT.Tanh)
         nc.sync.dma_start(out=out_1, in_=ct[:])
         backs_o = []
         for j in range(2):
-            backs_o.append(turn_back("o", j))
+            backs_o.append(turn_back(acts["o"], (2 * j, 2 * j + 1), "o%d" % j))
         for j, (lo, hi) in enumerate(halves):
-            nc.vector.tensor_tensor(out=pairs(ht[:, lo:hi]), in0=backs_o[j], in1=pairs(tanh_ct[:, lo:hi]), op=ALU.mult)
+            nc.vector.tensor_tensor(
+                out=units(ht[:, lo:hi], 2),
+                in0=backs_o[j][:].rearrange("b s n -> b n s"),
+                in1=units(tanh_ct[:, lo:hi], 2),
+                op=ALU.mult,
+            )
             nc.sync.dma_start(out=out_0[:, lo:hi], in_=ht[:, lo:hi])

@@ -19,7 +19,8 @@ ROWS = 4
 PLANES = 2
 GATES = 4
 IDLE_N = 256
-WARM_PASSES = 6
+WARM_MATMULS = 3
+WARM_PASSES = 3
 
 FLOPS = 2 * P * (K + K) * GATES * H
 
@@ -53,7 +54,9 @@ def tile_lstmcell_s_kernel(
         ident_f32 = keep.tile([P, P], F32)
         make_identity(nc, ident_f32[:])
         idle_values = keep.tile([P, IDLE_N * PACK], BF16, align_bytes=64)
-        nc.vector.memset(idle_values[:].bitcast(F32), 0.0)
+        idle_words = idle_values[:].bitcast(F32)
+        for half in range(2):
+            nc.vector.memset(idle_words[:, half * IDLE_N : (half + 1) * IDLE_N], 0.0)
         idle_codes = keep.tile([P, IDLE_N], U32, align_bytes=64)
         idle_scales = keep.tile([P, IDLE_N], U8, align_bytes=64)
         nc.vector.quantize_mx(out=idle_codes[:].bitcast(FP8X4), scales=idle_scales[:], in_=idle_values[:])
@@ -99,6 +102,16 @@ def tile_lstmcell_s_kernel(
         nc.sync.dma_start(out=cx_sb[:], in_=cx)
 
         gate_banks = {"f": psum_g.tile([P, ROWS, P], F32, tag="gate", name="gate_f")}
+
+        def idle_matmuls(count):
+            for i in range(count):
+                nc.tensor.matmul(
+                    out=gate_banks["f"][:].rearrange("p r n -> p (r n)"),
+                    lhsT=idle_values[:, 0:P],
+                    rhs=idle_values[:, 0:H],
+                    start=True,
+                    stop=True,
+                )
 
         def idle_passes(count):
             for i in range(count):
@@ -215,6 +228,7 @@ def tile_lstmcell_s_kernel(
             return tile_part.rearrange("b (n r) -> b n r", r=slots)
 
         every = range(ROWS)
+        idle_matmuls(WARM_MATMULS)
         idle_passes(WARM_PASSES)
         for m in range(n_matrices - 1):
             start_matrix(m)
@@ -227,7 +241,7 @@ def tile_lstmcell_s_kernel(
             if m == 0:
                 transpose_xh()
                 quantise_xh()
-            if m < 2:
+            if m < 3:
                 idle_passes(2)
             if m == 3:
                 multiply(0, every)

@@ -22,6 +22,8 @@ IDLE_N = 256
 WARM_MATMULS = 3
 WARM_PASSES = 3
 
+HALVED = ("i", "g", "o")
+
 FLOPS = 2 * P * (K + K) * GATES * H
 
 
@@ -75,7 +77,7 @@ def tile_lstmcell_s_kernel(
                 nc.sync.dma_start(out=x_sb[:], in_=xt)
                 h_sb = keep.tile([P, K], BF16)
                 nc.sync.dma_start(out=h_sb[:], in_=hx)
-            elif name == "o":
+            elif name in HALVED:
                 w_halves = w_sb[:].rearrange("p (j c) -> p j c", j=2)
                 source_halves = source.rearrange("(j p s) k -> p j (s k)", j=2, s=2)
                 if m < n_matrices - 1:
@@ -91,7 +93,7 @@ def tile_lstmcell_s_kernel(
             if m == 2:
                 for gate in gate_names:
                     b_cols[gate] = keep.tile([P, ROWS], BF16, name="b_%s" % gate)
-                    if gate == "o":
+                    if gate in HALVED:
                         nc.sync.dma_start(
                             out=b_cols[gate][:].rearrange("p (j s) -> p j s", j=2),
                             in_=gate_b[gate].rearrange("(j p s) -> p j s", j=2, s=2),
@@ -235,7 +237,7 @@ def tile_lstmcell_s_kernel(
             for first in (0, 2):
                 transpose_rows(m, first, 2)
             copy_rows(m, 0, 2, nc.scalar.copy)
-            copy_rows(m, 2, 2, nc.vector.tensor_copy if 0 < m < 6 else nc.scalar.copy)
+            copy_rows(m, 2, 2, nc.vector.tensor_copy if m > 0 else nc.scalar.copy)
             for first in (0, 2):
                 quantise_rows(m, first, 2)
             if m == 0:
@@ -249,13 +251,13 @@ def tile_lstmcell_s_kernel(
             if m == 5:
                 multiply(1, every)
                 activate(1, every)
-        back_f = turn_back(acts["f"], every, "f")
         last = n_matrices - 1
         start_matrix(last)
         transpose_rows(last, 0, 2)
         transpose_rows(last, 2, 1)
         transpose_rows(last, 3, 1)
         multiply(2, every)
+        back_f = turn_back(acts["f"], every, "f")
         copy_rows(last, 0, 2, nc.scalar.copy)
         copy_rows(last, 2, 1, nc.vector.tensor_copy)
         copy_rows(last, 3, 1, nc.scalar.copy)
@@ -263,24 +265,29 @@ def tile_lstmcell_s_kernel(
         quantise_rows(last, 0, 2)
         quantise_rows(last, 2, 1)
         quantise_rows(last, 3, 1)
-        for j in range(2):
+        for j, (lo, hi) in enumerate(halves):
             nc.vector.tensor_tensor(
                 out=product[:, 2 * j : 2 * j + 2, :],
                 in0=acts["i"][:, 2 * j : 2 * j + 2, :],
                 in1=acts["g"][:, 2 * j : 2 * j + 2, :],
                 op=ALU.mult,
             )
-        nc.vector.tensor_tensor(
-            out=units(kept[:], ROWS), in0=back_f[:].rearrange("b r n -> b n r"), in1=units(cx_sb[:], ROWS), op=ALU.mult
-        )
+            nc.vector.tensor_tensor(
+                out=units(kept[:, lo:hi], ROWS),
+                in0=back_f[:, :, lo // ROWS : hi // ROWS].rearrange("b r n -> b n r"),
+                in1=units(cx_sb[:, lo:hi], ROWS),
+                op=ALU.mult,
+            )
         multiply(3, (0, 1))
         multiply(3, (2, 3))
-        back_p = turn_back(product, every, "p")
+        backs_p = []
+        for j in range(2):
+            backs_p.append(turn_back(product, (2 * j, 2 * j + 1), "p%d" % j))
         for j, (lo, hi) in enumerate(halves):
             nc.vector.tensor_tensor(
-                out=units(ct[:, lo:hi], ROWS),
-                in0=back_p[:, :, lo // ROWS : hi // ROWS].rearrange("b r n -> b n r"),
-                in1=units(kept[:, lo:hi], ROWS),
+                out=units(ct[:, lo:hi], 2),
+                in0=backs_p[j][:].rearrange("b s n -> b n s"),
+                in1=units(kept[:, lo:hi], 2),
                 op=ALU.add,
             )
         activate(3, every)
@@ -290,10 +297,12 @@ def tile_lstmcell_s_kernel(
         backs_o = []
         for j in range(2):
             backs_o.append(turn_back(acts["o"], (2 * j, 2 * j + 1), "o%d" % j))
-        for j, (lo, hi) in enumerate(halves):
+        for j, first, count in ((0, 0, P), (1, 0, P // 2), (1, P // 2, P // 2)):
+            lo = j * (H // 2) + 2 * first
+            hi = lo + 2 * count
             nc.vector.tensor_tensor(
                 out=units(ht[:, lo:hi], 2),
-                in0=backs_o[j][:].rearrange("b s n -> b n s"),
+                in0=backs_o[j][:, :, first : first + count].rearrange("b s n -> b n s"),
                 in1=units(tanh_ct[:, lo:hi], 2),
                 op=ALU.mult,
             )

@@ -22,8 +22,6 @@ IDLE_N = 256
 WARM_MATMULS = 3
 WARM_PASSES = 3
 
-HALVED = ("i", "g", "o")
-
 FLOPS = 2 * P * (K + K) * GATES * H
 
 
@@ -62,44 +60,35 @@ def tile_lstmcell_s_kernel(
         idle_codes = keep.tile([P, IDLE_N], U32, align_bytes=64)
         idle_scales = keep.tile([P, IDLE_N], U8, align_bytes=64)
         nc.vector.quantize_mx(out=idle_codes[:].bitcast(FP8X4), scales=idle_scales[:], in_=idle_values[:])
+        b_rows = keep.tile([P, H], BF16)
+        nc.vector.memset(b_rows[:].bitcast(F32), 0.0)
+
         weights_sb = []
-        b_cols = {}
         for m, (kind, name, source) in enumerate(matrices):
             w_sb = keep.tile([P, ROWS * K], BF16, name="%s_%s_sb" % (kind, name))
             weights_sb.append(w_sb)
+            w_halves = w_sb[:].rearrange("p (j c) -> p j c", j=2)
+            source_halves = source.rearrange("(j p s) k -> p j (s k)", j=2, s=2)
             if m == 0:
                 for j in range(2):
-                    nc.sync.dma_start(
-                        out=w_sb[:].rearrange("p (r k) -> p r k", r=ROWS)[:, 2 * j : 2 * j + 2, :],
-                        in_=source.rearrange("(p r) k -> p r k", r=ROWS)[:, 2 * j : 2 * j + 2, :],
-                    )
+                    nc.sync.dma_start(out=w_halves[:, j, :], in_=source_halves[:, j, :])
                 x_sb = keep.tile([P, K], BF16)
                 nc.sync.dma_start(out=x_sb[:], in_=xt)
                 h_sb = keep.tile([P, K], BF16)
                 nc.sync.dma_start(out=h_sb[:], in_=hx)
-            elif name in HALVED:
-                w_halves = w_sb[:].rearrange("p (j c) -> p j c", j=2)
-                source_halves = source.rearrange("(j p s) k -> p j (s k)", j=2, s=2)
-                if m < n_matrices - 1:
-                    nc.sync.dma_start(out=w_halves, in_=source_halves)
-                else:
-                    nc.sync.dma_start(out=w_halves[:, 0, :], in_=source_halves[:, 0, :])
-                    for s in range(2):
-                        nc.sync.dma_start(
-                            out=w_halves[:, 1, s * K : (s + 1) * K], in_=source_halves[:, 1, s * K : (s + 1) * K]
-                        )
+            elif m < n_matrices - 1:
+                nc.sync.dma_start(out=w_halves, in_=source_halves)
             else:
-                nc.sync.dma_start(out=w_sb[:], in_=source.rearrange("(p r) k -> p (r k)", r=ROWS))
-            if m == 2:
-                for gate in gate_names:
-                    b_cols[gate] = keep.tile([P, ROWS], BF16, name="b_%s" % gate)
-                    if gate in HALVED:
-                        nc.sync.dma_start(
-                            out=b_cols[gate][:].rearrange("p (j s) -> p j s", j=2),
-                            in_=gate_b[gate].rearrange("(j p s) -> p j s", j=2, s=2),
-                        )
-                    else:
-                        nc.sync.dma_start(out=b_cols[gate][:], in_=gate_b[gate].rearrange("(p r) -> p r", r=ROWS))
+                nc.sync.dma_start(out=w_halves[:, 0, :], in_=source_halves[:, 0, :])
+                for s in range(2):
+                    nc.sync.dma_start(
+                        out=w_halves[:, 1, s * K : (s + 1) * K], in_=source_halves[:, 1, s * K : (s + 1) * K]
+                    )
+            if m == 3:
+                for index, gate in enumerate(gate_names):
+                    nc.sync.dma_start(
+                        out=b_rows[index : index + 1, :], in_=gate_b[gate].rearrange("(c j) -> c j", c=1)
+                    )
         cx_sb = keep.tile([P, H], BF16)
         nc.sync.dma_start(out=cx_sb[:], in_=cx)
 
@@ -210,14 +199,24 @@ def tile_lstmcell_s_kernel(
                         stop=(kind == "r"),
                     )
 
+        b_cols = keep.tile([P, 2, GATES], F32)
+
+        def bias_columns():
+            bank = psum_t.tile([P, 2, P], F32, tag="bank", name="bias_bank")
+            for j in range(2):
+                nc.tensor.transpose(bank[:, j, :], b_rows[:].bitcast(F32)[:, j * P : (j + 1) * P], ident_f32[:])
+            nc.scalar.copy(out=b_cols[:], in_=bank[:, :, 0:GATES])
+
         def activate(index, slots):
             name = gate_names[index]
+            biases = b_cols[:].rearrange("p j g -> p (j g)").bitcast(BF16)
             for c in slots:
+                column = (c // 2 * GATES + index) * 2 + c % 2
                 nc.scalar.activation(
                     out=acts[name][:, c, :],
                     in_=gate_banks[name][:, c, :],
                     func=gate_func[name],
-                    bias=b_cols[name][:, c : c + 1],
+                    bias=biases[:, column : column + 1],
                 )
 
         def turn_back(source, slots, label):
@@ -247,6 +246,8 @@ def tile_lstmcell_s_kernel(
                 idle_passes(2)
             if m == 3:
                 multiply(0, every)
+            if m == 4:
+                bias_columns()
                 activate(0, every)
             if m == 5:
                 multiply(1, every)
@@ -273,9 +274,9 @@ def tile_lstmcell_s_kernel(
                 op=ALU.mult,
             )
             nc.vector.tensor_tensor(
-                out=units(kept[:, lo:hi], ROWS),
-                in0=back_f[:, :, lo // ROWS : hi // ROWS].rearrange("b r n -> b n r"),
-                in1=units(cx_sb[:, lo:hi], ROWS),
+                out=units(kept[:, lo:hi], 2),
+                in0=back_f[:, 2 * j : 2 * j + 2, :].rearrange("b s n -> b n s"),
+                in1=units(cx_sb[:, lo:hi], 2),
                 op=ALU.mult,
             )
         multiply(3, (0, 1))

from contextlib import ExitStack

import concourse.mybir as mybir
from concourse.masks import make_identity

F32 = mybir.dt.float32
BF16 = mybir.dt.bfloat16
U32 = mybir.dt.uint32
U8 = mybir.dt.uint8
FP8X4 = mybir.dt.float8_e4m3fn_x4
ACT = mybir.ActivationFunctionType
ALU = mybir.AluOpType

P = 128
K = 512
H = 512
PACK = 4
ROWS = 4
PLANES = 2
GATES = 4
IDLE_N = 256
WARM_MATMULS = 3
WARM_PASSES = 3

FLOPS = 2 * P * (K + K) * GATES * H


def tile_lstmcell_s_kernel(
    tc, xt, cx, hx, w_fg, w_ig, w_og, w_ci, r_fg, r_ig, r_og, r_ci, b_fg, b_ig, b_og, b_ci, out_0, out_1
):
    nc = tc.nc
    gate_names = ["f", "i", "g", "o"]
    gate_w = {"f": w_fg, "i": w_ig, "g": w_ci, "o": w_og}
    gate_r = {"f": r_fg, "i": r_ig, "g": r_ci, "o": r_og}
    gate_b = {"f": b_fg, "i": b_ig, "g": b_ci, "o": b_og}
    gate_func = {"f": ACT.Sigmoid, "i": ACT.Sigmoid, "g": ACT.Tanh, "o": ACT.Sigmoid}
    matrices = []
    for name in gate_names:
        matrices.append(("w", name, gate_w[name]))
        matrices.append(("r", name, gate_r[name]))
    n_matrices = len(matrices)

    with ExitStack() as ctx:
        keep = ctx.enter_context(tc.tile_pool(name="keep", bufs=1))
        stage = ctx.enter_context(tc.tile_pool(name="stage", bufs=4))
        psum_t = ctx.enter_context(tc.psum_pool(name="psum_t", bufs=6))
        psum_g = ctx.enter_context(tc.psum_pool(name="psum_g", bufs=2))
        ctx.enter_context(tc.manual_schedule())

        warm_in = keep.tile([P, 1], F32)
        nc.gpsimd.memset(warm_in[:], 0.0)
        warm_out = keep.tile([P, 1], F32)
        nc.scalar.activation(out=warm_out[:], in_=warm_in[:], func=ACT.Sigmoid)
        ident_f32 = keep.tile([P, P], F32)
        make_identity(nc, ident_f32[:])
        idle_values = keep.tile([P, IDLE_N * PACK], BF16, align_bytes=64)
        idle_words = idle_values[:].bitcast(F32)
        for half in range(2):
            nc.vector.memset(idle_words[:, half * IDLE_N : (half + 1) * IDLE_N], 0.0)
        idle_codes = keep.tile([P, IDLE_N], U32, align_bytes=64)
        idle_scales = keep.tile([P, IDLE_N], U8, align_bytes=64)
        nc.vector.quantize_mx(out=idle_codes[:].bitcast(FP8X4), scales=idle_scales[:], in_=idle_values[:])
        b_rows = keep.tile([P, H], BF16)
        nc.vector.memset(b_rows[:].bitcast(F32), 0.0)

        weights_sb = []
        for m, (kind, name, source) in enumerate(matrices):
            w_sb = keep.tile([P, ROWS * K], BF16, name="%s_%s_sb" % (kind, name))
            weights_sb.append(w_sb)
            w_halves = w_sb[:].rearrange("p (j c) -> p j c", j=2)
            source_halves = source.rearrange("(j p s) k -> p j (s k)", j=2, s=2)
            if m == 0:
                for j in range(2):
                    nc.sync.dma_start(out=w_halves[:, j, :], in_=source_halves[:, j, :])
                x_sb = keep.tile([P, K], BF16)
                nc.sync.dma_start(out=x_sb[:], in_=xt)
                h_sb = keep.tile([P, K], BF16)
                nc.sync.dma_start(out=h_sb[:], in_=hx)
            elif m < n_matrices - 1:
                nc.sync.dma_start(out=w_halves, in_=source_halves)
            else:
                nc.sync.dma_start(out=w_halves[:, 0, :], in_=source_halves[:, 0, :])
                for s in range(2):
                    nc.sync.dma_start(
                        out=w_halves[:, 1, s * K : (s + 1) * K], in_=source_halves[:, 1, s * K : (s + 1) * K]
                    )
            if m == 3:
                for index, gate in enumerate(gate_names):
                    nc.sync.dma_start(
                        out=b_rows[index : index + 1, :], in_=gate_b[gate].rearrange("(c j) -> c j", c=1)
                    )
        cx_sb = keep.tile([P, H], BF16)
        nc.sync.dma_start(out=cx_sb[:], in_=cx)

        gate_banks = {"f": psum_g.tile([P, ROWS, P], F32, tag="gate", name="gate_f")}

        def idle_matmuls(count):
            for i in range(count):
                nc.tensor.matmul(
                    out=gate_banks["f"][:].rearrange("p r n -> p (r n)"),
                    lhsT=idle_values[:, 0:P],
                    rhs=idle_values[:, 0:H],
                    start=True,
                    stop=True,
                )

        def idle_passes(count):
            for i in range(count):
                nc.tensor.matmul_mx(
                    out=gate_banks["f"][:, 0 : IDLE_N // P, :].rearrange("p r n -> p (r n)"),
                    lhsT=idle_codes[:, 0:P].bitcast(FP8X4),
                    lhsT_scale=idle_scales[:, 0:P],
                    rhs=idle_codes[:].bitcast(FP8X4),
                    rhs_scale=idle_scales[:],
                    start=True,
                    stop=True,
                )

        def transpose_words(bank, slot, u, source_sb, first_word):
            nc.tensor.transpose(
                bank[:, slot, u, :],
                source_sb[:].bitcast(F32)[:, first_word : first_word + P],
                ident_f32[:],
            )

        xh_grouped = keep.tile([P, 2 * P * PACK], BF16, align_bytes=64)
        xh_codes = keep.tile([P, 2 * P], U32, align_bytes=64)
        xh_scales = keep.tile([P, 2 * P], U8, align_bytes=64)
        batch_cols = {"w": slice(0, P), "r": slice(P, 2 * P)}

        def transpose_xh():
            xh_bank = psum_t.tile([P, 2, PLANES, P], F32, tag="bank")
            for s, source_sb in enumerate((x_sb, h_sb)):
                for u in range(PLANES):
                    transpose_words(xh_bank, s, u, source_sb, u * P)
            nc.scalar.copy(
                out=xh_grouped[:].bitcast(F32).rearrange("p (s n u) -> p s n u", s=2, u=PLANES),
                in_=xh_bank[:].rearrange("p s u n -> p s n u"),
            )

        def quantise_xh():
            nc.vector.quantize_mx(out=xh_codes[:].bitcast(FP8X4), scales=xh_scales[:], in_=xh_grouped[:])

        grouped_tiles = {}
        codes_tiles = {}
        scales_tiles = {}
        acts = {}
        banks = {}

        def start_matrix(m):
            grouped_tiles[m] = stage.tile([P, H * PACK], BF16, align_bytes=64, tag="grouped", name="grouped_%d" % m)
            codes_tiles[m] = keep.tile([P, H], U32, align_bytes=64, name="codes_%d" % m)
            scales_tiles[m] = keep.tile([P, H], U8, align_bytes=64, name="scales_%d" % m)

        def transpose_rows(m, first, count):
            bank = psum_t.tile([P, count, PLANES, P], F32, tag="bank", name="bank_%d_%d" % (m, first))
            for s in range(count):
                for u in range(PLANES):
                    transpose_words(bank, s, u, weights_sb[m], (first + s) * (K // 2) + u * P)
            banks[m, first] = bank

        def copy_rows(m, first, count, copy):
            words = grouped_tiles[m][:].bitcast(F32).rearrange("p (r n u) -> p r n u", r=ROWS, u=PLANES)
            copy(
                out=words[:, first : first + count, :, :],
                in_=banks[m, first][:].rearrange("p s u n -> p s n u"),
            )

        def quantise_rows(m, first, count):
            lo, hi = first * P, (first + count) * P
            nc.vector.quantize_mx(
                out=codes_tiles[m][:, lo:hi].bitcast(FP8X4),
                scales=scales_tiles[m][:, lo:hi],
                in_=grouped_tiles[m][:, lo * PACK : hi * PACK],
            )

        halves = [(0, H // 2), (H // 2, H)]
        for name in gate_names:
            acts[name] = keep.tile([P, ROWS, P], F32, name="act_%s" % name)
        product = keep.tile([P, ROWS, P], F32)
        kept = keep.tile([P, H], F32)
        ct = keep.tile([P, H], F32)
        tanh_ct = keep.tile([P, H], F32)
        ht = keep.tile([P, H], F32)

        def multiply(index, slots):
            name = gate_names[index]
            if name not in gate_banks:
                gate_banks[name] = psum_g.tile([P, ROWS, P], F32, tag="gate", name="gate_%s" % name)
            for c in slots:
                for kind, m in (("w", 2 * index), ("r", 2 * index + 1)):
                    nc.tensor.matmul_mx(
                        out=gate_banks[name][:, c, :],
                        lhsT=codes_tiles[m][:, c * P : (c + 1) * P].bitcast(FP8X4),
                        lhsT_scale=scales_tiles[m][:, c * P : (c + 1) * P],
                        rhs=xh_codes[:, batch_cols[kind]].bitcast(FP8X4),
                        rhs_scale=xh_scales[:, batch_cols[kind]],
                        start=(kind == "w"),
                        stop=(kind == "r"),
                    )

        b_cols = keep.tile([P, 2, GATES], F32)

        def bias_columns():
            bank = psum_t.tile([P, 2, P], F32, tag="bank", name="bias_bank")
            for j in range(2):
                nc.tensor.transpose(bank[:, j, :], b_rows[:].bitcast(F32)[:, j * P : (j + 1) * P], ident_f32[:])
            nc.scalar.copy(out=b_cols[:], in_=bank[:, :, 0:GATES])

        def activate(index, slots):
            name = gate_names[index]
            biases = b_cols[:].rearrange("p j g -> p (j g)").bitcast(BF16)
            for c in slots:
                column = (c // 2 * GATES + index) * 2 + c % 2
                nc.scalar.activation(
                    out=acts[name][:, c, :],
                    in_=gate_banks[name][:, c, :],
                    func=gate_func[name],
                    bias=biases[:, column : column + 1],
                )

        def turn_back(source, slots, label):
            bank = psum_t.tile([P, len(slots), P], F32, tag="bank", name="back_%s" % label)
            for i, c in enumerate(slots):
                nc.tensor.transpose(bank[:, i, :], source[:, c, :], ident_f32[:])
            return bank

        def units(tile_part, slots):
            return tile_part.rearrange("b (n r) -> b n r", r=slots)

        every = range(ROWS)
        idle_matmuls(WARM_MATMULS)
        idle_passes(WARM_PASSES)
        for m in range(n_matrices - 1):
            start_matrix(m)
            for first in (0, 2):
                transpose_rows(m, first, 2)
            copy_rows(m, 0, 2, nc.scalar.copy)
            copy_rows(m, 2, 2, nc.vector.tensor_copy if m > 0 else nc.scalar.copy)
            for first in (0, 2):
                quantise_rows(m, first, 2)
            if m == 0:
                transpose_xh()
                quantise_xh()
            if m < 3:
                idle_passes(2)
            if m == 3:
                multiply(0, every)
            if m == 4:
                bias_columns()
                activate(0, every)
            if m == 5:
                multiply(1, every)
                activate(1, every)
        last = n_matrices - 1
        start_matrix(last)
        transpose_rows(last, 0, 2)
        transpose_rows(last, 2, 1)
        transpose_rows(last, 3, 1)
        multiply(2, every)
        back_f = turn_back(acts["f"], every, "f")
        copy_rows(last, 0, 2, nc.scalar.copy)
        copy_rows(last, 2, 1, nc.vector.tensor_copy)
        copy_rows(last, 3, 1, nc.scalar.copy)
        activate(2, every)
        quantise_rows(last, 0, 2)
        quantise_rows(last, 2, 1)
        quantise_rows(last, 3, 1)
        for j, (lo, hi) in enumerate(halves):
            nc.vector.tensor_tensor(
                out=product[:, 2 * j : 2 * j + 2, :],
                in0=acts["i"][:, 2 * j : 2 * j + 2, :],
                in1=acts["g"][:, 2 * j : 2 * j + 2, :],
                op=ALU.mult,
            )
            nc.vector.tensor_tensor(
                out=units(kept[:, lo:hi], 2),
                in0=back_f[:, 2 * j : 2 * j + 2, :].rearrange("b s n -> b n s"),
                in1=units(cx_sb[:, lo:hi], 2),
                op=ALU.mult,
            )
        multiply(3, (0, 1))
        multiply(3, (2, 3))
        backs_p = []
        for j in range(2):
            backs_p.append(turn_back(product, (2 * j, 2 * j + 1), "p%d" % j))
        for j, (lo, hi) in enumerate(halves):
            nc.vector.tensor_tensor(
                out=units(ct[:, lo:hi], 2),
                in0=backs_p[j][:].rearrange("b s n -> b n s"),
                in1=units(kept[:, lo:hi], 2),
                op=ALU.add,
            )
        activate(3, every)
        for j, (lo, hi) in enumerate(halves):
            nc.scalar.activation(out=tanh_ct[:, lo:hi], in_=ct[:, lo:hi], func=ACT.Tanh)
        nc.sync.dma_start(out=out_1, in_=ct[:])
        backs_o = []
        for j in range(2):
            backs_o.append(turn_back(acts["o"], (2 * j, 2 * j + 1), "o%d" % j))
        for j, first, count in ((0, 0, P), (1, 0, P // 2), (1, P // 2, P // 2)):
            lo = j * (H // 2) + 2 * first
            hi = lo + 2 * count
            nc.vector.tensor_tensor(
                out=units(ht[:, lo:hi], 2),
                in0=backs_o[j][:, :, first : first + count].rearrange("b s n -> b n s"),
                in1=units(tanh_ct[:, lo:hi], 2),
                op=ALU.mult,
            )
            nc.sync.dma_start(out=out_0[:, lo:hi], in_=ht[:, lo:hi])
